import numpy as np
import ml_dtypes


def mxq(x, axis, fmt="e4m3"):
    dtype, down = {"e4m3": (ml_dtypes.float8_e4m3fn, 7), "e5m2": (ml_dtypes.float8_e5m2, 14)}[fmt]
    v = np.moveaxis(np.asarray(x, np.float32).astype(ml_dtypes.bfloat16).astype(np.float64), axis, -1)
    blocks = v.reshape(v.shape[:-1] + (-1, 32))
    amax = np.abs(blocks).max(-1, keepdims=True)
    byte = np.maximum(np.where(amax > 0, np.frexp(amax)[1] - 1 + 127, 0) - down, 1)
    scale = np.exp2(byte - 127.0)
    codes = (blocks / scale).astype(np.float32).astype(dtype).astype(np.float64)
    return np.moveaxis((codes * scale).reshape(v.shape), -1, axis)


WIDE = False


def mx_kscale(k):
    if not WIDE:
        return np.ones(k)
    levels = np.array([10, -10, 5, -5, 0])
    if k % 512:
        return np.exp2(np.random.permutation(np.resize(levels, k // 32))).repeat(32)
    a = np.empty((k // 512, 16))
    for p in range(k // 512):
        a[p, :8] = np.random.permutation(np.resize(levels, 8))
        for g in range(8):
            far = levels[np.abs(levels - a[p, g]) >= 10]
            a[p, g + 8] = far[np.random.randint(len(far))]
    return np.exp2(a.ravel()).repeat(32)


BF16 = ml_dtypes.bfloat16


def bf(x):
    return np.asarray(x, np.float32).astype(BF16)


def f64(x):
    return np.asarray(x).astype(np.float64)


B, G, D, H, DH, R, F, L = 1, 32, 1024, 4, 512, 200, 4096, 2
S = G * G
INNER = H * DH
ROT = 2 * R
MAX_FREQ = 10.0
EPS = 1e-5


def make_freqs():
    exps = np.linspace(0.0, np.log(MAX_FREQ / 2.0) / np.log(2.0), R // 2)
    base = (2.0 ** exps) * np.pi
    t = np.linspace(-1.0, 1.0, G)
    f = np.repeat(t[:, None] * base[None, :], 2, axis=-1)
    fh = np.broadcast_to(f[:, None, :], (G, G, R))
    fw = np.broadcast_to(f[None, :, :], (G, G, R))
    return np.concatenate([fh, fw], axis=-1)


def rotate_half(u):
    u = u.reshape(u.shape[:-1] + (u.shape[-1] // 2, 2))
    return np.concatenate([-u[..., 1], u[..., 0]], axis=-1)


def apply_rot(t, cosf, sinf):
    tb = t.reshape(B, H, G, G, DH)
    tl, tr = tb[..., :ROT], tb[..., ROT:]
    tl = tl * cosf + rotate_half(tl) * sinf
    return np.concatenate([tl, tr], axis=-1).reshape(B, H, S, DH)


def to_heads(t):
    return t.reshape(B, S, H, DH).transpose(0, 2, 1, 3)


def setup_inputs():
    s = mx_kscale(D)
    return {'x_grid': bf(np.random.standard_normal((B, S, D))),
            'ln_g': bf((1.0 + 0.1 * np.random.standard_normal(D)) * s),
            'ln_b': bf(0.1 * np.random.standard_normal(D) * s),
            'w_qk': bf(np.random.standard_normal((D, 2 * INNER)) * 1.5 / np.sqrt(D) / s[:, None])}


def reference(x_grid, ln_g, ln_b, w_qk):
    x = f64(x_grid)
    mu = np.mean(x, axis=-1, keepdims=True)
    var = np.mean(np.square(x - mu), axis=-1, keepdims=True)
    xn = (x - mu) / np.sqrt(var + EPS) * f64(ln_g) + f64(ln_b)
    qk = mxq(xn, 2, 'e4m3') @ mxq(f64(w_qk), 0, 'e4m3')
    q, k = to_heads(qk[..., :INNER]), to_heads(qk[..., INNER:])
    freqs = make_freqs()
    cosf, sinf = np.cos(freqs)[None, None], np.sin(freqs)[None, None]
    return apply_rot(q, cosf, sinf), apply_rot(k, cosf, sinf)

@@ -1,0 +1,297 @@
+import math
+from contextlib import ExitStack
+
+import concourse.mybir as mybir
+from concourse.masks import make_identity
+
+F32 = mybir.dt.float32
+BF16 = mybir.dt.bfloat16
+I32 = mybir.dt.int32
+U32 = mybir.dt.uint32
+U8 = mybir.dt.uint8
+FP8X4 = mybir.dt.float8_e4m3fn_x4
+ALU = mybir.AluOpType
+ACT = mybir.ActivationFunctionType
+
+P = 128
+GRID = 32
+TOKENS = GRID * GRID
+FEATURES = 1024
+HEADS = 8
+HEADS_PER_OUTPUT = 4
+CHANNELS = 512
+FREQS = 100
+HALF = 2 * FREQS
+ROTATED = 2 * HALF
+MAX_FREQ = 10.0
+EPS = 1e-5
+
+PACK = 4
+K_PASS = P * PACK
+PASSES = FEATURES // K_PASS
+CHUNKS = FEATURES // P
+TILES = TOKENS // P
+GROUP = 4
+GROUPS = TILES // GROUP
+GROUP_TOKENS = GROUP * P
+BN_WIDTH = 512
+
+QUARTERS = 4
+PIECE_CHANNELS = CHANNELS // QUARTERS
+W_PIECES = PASSES * QUARTERS
+W_LEAD = W_PIECES + 2
+W_BUFS = 3
+
+ROUND_MAGIC = 12582912.0
+
+FLOPS = 2 * TOKENS * FEATURES * HEADS * CHANNELS
+
+
+def regroup(copy, grouped, planes):
+    copy(
+        out=grouped.rearrange("p (c i) t -> p c t i", i=4),
+        in_=planes.rearrange("p t (c i) -> p c t i", i=4),
+    )
+
+
+def tile_transformerencoderlayer_pa_kernel(tc, x_grid, ln_g, ln_b, w_qk, out_0, out_1):
+    nc = tc.nc
+    with ExitStack() as ctx:
+        keep = ctx.enter_context(tc.tile_pool(name="keep", bufs=1))
+        small = ctx.enter_context(tc.tile_pool(name="small", bufs=TILES))
+        hat_pool = ctx.enter_context(tc.tile_pool(name="hat", bufs=2))
+        stage = ctx.enter_context(tc.tile_pool(name="stage", bufs=2))
+        grouped_pool = ctx.enter_context(tc.tile_pool(name="grouped", bufs=2))
+        w_pool = ctx.enter_context(tc.tile_pool(name="w", bufs=W_BUFS))
+        y_pool = ctx.enter_context(tc.tile_pool(name="y", bufs=5))
+        cross_pool = ctx.enter_context(tc.tile_pool(name="cross", bufs=3))
+        flip_psum = ctx.enter_context(tc.psum_pool(name="flip", bufs=2))
+        acc_psum = ctx.enter_context(tc.psum_pool(name="acc", bufs=6))
+
+        gain_raw = keep.tile([P, PASSES, PACK], BF16)
+        bias_raw = keep.tile([P, PASSES, PACK], BF16)
+        nc.sync.dma_start(out=gain_raw[:], in_=ln_g.rearrange("(g p t) -> p g t", p=P, t=PACK))
+        nc.sync.dma_start(out=bias_raw[:], in_=ln_b.rearrange("(g p t) -> p g t", p=P, t=PACK))
+
+        x_sb = keep.tile([P, TILES, FEATURES], BF16)
+        x_view = x_grid[0].rearrange("(p i) d -> p i d", i=TILES)
+
+        def load_x(group):
+            for pair in range(group * GROUP, (group + 1) * GROUP, 2):
+                nc.sync.dma_start(out=x_sb[:, pair : pair + 2, :], in_=x_view[:, pair : pair + 2, :])
+
+        w_view = w_qk.rearrange("(g p t) n -> p g t n", t=PACK, p=P)
+
+        w_raw = {}
+
+        def load_w(head):
+            w_raw[head] = w_pool.tile([P, PASSES, PACK, CHANNELS], BF16, name="w_raw")
+            for g in range(PASSES):
+                nc.sync.dma_start(
+                    out=w_raw[head][:, g], in_=w_view[:, g, :, head * CHANNELS : (head + 1) * CHANNELS]
+                )
+
+        load_x(0)
+        load_w(0)
+        load_x(1)
+        for head in range(1, W_BUFS):
+            load_w(head)
+
+        token = keep.tile([P, TILES], I32)
+        nc.gpsimd.iota(token[:], pattern=[[1, TILES]], base=0, channel_multiplier=TILES)
+
+        freq = keep.tile([P, P], F32)
+        ratio = (MAX_FREQ / 2.0) ** (1.0 / (FREQS - 1))
+        nc.vector.memset(freq[:, 0:1], 0.5)
+        for doubling in range(7):
+            filled = 2**doubling
+            nc.vector.tensor_scalar_mul(
+                out=freq[:, filled : 2 * filled], in0=freq[:, 0:filled], scalar1=ratio**filled
+            )
+
+        minus_half = keep.tile([P, 1], F32)
+        nc.gpsimd.memset(minus_half[:], -0.5)
+        ident = keep.tile([P, P], F32)
+        make_identity(nc, ident[:])
+
+        gain_bias = keep.tile([P, 2 * CHUNKS], F32)
+        nc.vector.tensor_copy(out=gain_bias[:, 0:CHUNKS], in_=gain_raw[:].rearrange("p g t -> p (g t)"))
+        nc.vector.tensor_copy(out=gain_bias[:, CHUNKS : 2 * CHUNKS], in_=bias_raw[:].rearrange("p g t -> p (g t)"))
+
+        xn_t = keep.tile([P, CHUNKS, TOKENS], BF16)
+        x_codes = keep.tile([P, PASSES, TOKENS], U32, align_bytes=64)
+        x_scales = keep.tile([P, PASSES, TOKENS], U8, align_bytes=64)
+
+        def layer_norm_group(group):
+            group_cols = slice(group * GROUP_TOKENS, (group + 1) * GROUP_TOKENS)
+            x_hat = hat_pool.tile([P, GROUP, PASSES, PACK, P], F32)
+            for a in range(GROUP):
+                x_tile = x_sb[:, group * GROUP + a, :]
+                stats = small.tile([P, FEATURES // BN_WIDTH, 6], F32)
+                for part in range(FEATURES // BN_WIDTH):
+                    nc.vector.bn_stats(out=stats[:, part, :], in_=x_tile[:, part * BN_WIDTH : (part + 1) * BN_WIDTH])
+                mean_var = small.tile([P, 2], F32)
+                nc.vector.bn_aggr(out=mean_var[:], in_=stats[:].rearrange("p a s -> p (a s)"))
+                neg_mean = small.tile([P, 1], F32)
+                nc.vector.tensor_scalar_mul(out=neg_mean[:], in0=mean_var[:, 0:1], scalar1=-1.0)
+                var_eps = small.tile([P, 1], F32)
+                nc.vector.tensor_scalar_add(out=var_eps[:], in0=mean_var[:, 1:2], scalar1=EPS)
+                rstd = small.tile([P, 1], F32)
+                nc.gpsimd.tensor_tensor(out=rstd[:], in0=var_eps[:], in1=minus_half[:], op=ALU.pow)
+                nc.vector.tensor_scalar(
+                    out=x_hat[:, a],
+                    in0=x_tile.rearrange("m (g p t) -> m g t p", g=PASSES, t=PACK),
+                    scalar1=neg_mean[:],
+                    scalar2=rstd[:],
+                    op0=ALU.add,
+                    op1=ALU.mult,
+                )
+
+            for c in range(CHUNKS):
+                flipped = flip_psum.tile([P, GROUP, P], F32, tag="flipped")
+                for a in range(GROUP):
+                    nc.tensor.transpose(flipped[:, a, :], x_hat[:, a, c // PACK, c % PACK, :], ident[:])
+                nc.scalar.activation(
+                    out=xn_t[:, c, group_cols],
+                    in_=flipped[:].rearrange("p a m -> p (a m)"),
+                    func=ACT.Identity,
+                    scale=gain_bias[:, c : c + 1],
+                    bias=gain_bias[:, CHUNKS + c : CHUNKS + c + 1],
+                )
+
+            for g in range(PASSES):
+                xn_grouped = stage.tile([P, GROUP_TOKENS, PACK], BF16, align_bytes=64)
+                regroup(nc.vector.tensor_copy, xn_grouped[:], xn_t[:, g * PACK : (g + 1) * PACK, group_cols])
+                nc.vector.quantize_mx(
+                    out=x_codes[:, g, group_cols].bitcast(FP8X4),
+                    scales=x_scales[:, g, group_cols],
+                    in_=xn_grouped[:].rearrange("p c t -> p (c t)"),
+                )
+
+        w_grouped = {}
+        w_codes = {}
+        w_scales = {}
+
+        def prepare_w_piece(number):
+            head, piece = divmod(number, W_PIECES)
+            g, quarter = divmod(piece, QUARTERS)
+            piece_cols = slice(quarter * PIECE_CHANNELS, (quarter + 1) * PIECE_CHANNELS)
+            if piece == 0:
+                w_grouped[head] = grouped_pool.tile(
+                    [P, PASSES, CHANNELS, PACK], BF16, align_bytes=64, name="w_grouped"
+                )
+            regroup(nc.scalar.copy, w_grouped[head][:, g, piece_cols, :], w_raw[head][:, g, :, piece_cols])
+            if piece == W_PIECES - 1:
+                w_codes[head] = w_pool.tile([P, PASSES, CHANNELS], U32, align_bytes=64, name="w_codes")
+                w_scales[head] = w_pool.tile([P, PASSES, CHANNELS], U8, align_bytes=64, name="w_scales")
+                nc.vector.quantize_mx(
+                    out=w_codes[head][:].rearrange("p g c -> p (g c)").bitcast(FP8X4),
+                    scales=w_scales[head][:].rearrange("p g c -> p (g c)"),
+                    in_=w_grouped[head][:].rearrange("p g c t -> p (g c t)"),
+                )
+                if head + W_BUFS < HEADS:
+                    load_w(head + W_BUFS)
+
+        layer_norm_group(0)
+        for number in range(W_LEAD):
+            prepare_w_piece(number)
+
+        blocks = TILES + 1
+        grid_index = keep.tile([P, blocks], I32)
+        nc.vector.tensor_single_scalar(out=grid_index[:, 0:TILES], in_=token[:], scalar=GRID - 1, op=ALU.bitwise_and)
+        nc.vector.tensor_single_scalar(
+            out=grid_index[:, TILES:blocks], in_=token[:, 0:1], scalar=5, op=ALU.arith_shift_right
+        )
+        coord = keep.tile([P, blocks], F32)
+        nc.vector.tensor_scalar(
+            out=coord[:], in0=grid_index[:], scalar1=2.0 / (GRID - 1), scalar2=-1.0, op0=ALU.mult, op1=ALU.add
+        )
+        turn = keep.tile([P, blocks, FREQS], F32)
+        nc.vector.tensor_tensor(
+            out=turn[:],
+            in0=freq[:, 0:FREQS].unsqueeze(1).to_broadcast([P, blocks, FREQS]),
+            in1=coord[:].unsqueeze(2).to_broadcast([P, blocks, FREQS]),
+            op=ALU.mult,
+        )
+        rounded = keep.tile([P, blocks, FREQS], F32)
+        nc.vector.tensor_scalar_add(out=rounded[:], in0=turn[:], scalar1=ROUND_MAGIC)
+        back = keep.tile([P, blocks, FREQS], F32)
+        nc.vector.scalar_tensor_tensor(
+            out=back[:].rearrange("p b j -> p (b j)"),
+            in0=rounded[:].rearrange("p b j -> p (b j)"),
+            scalar=ROUND_MAGIC,
+            in1=turn[:].rearrange("p b j -> p (b j)"),
+            op0=ALU.subtract,
+            op1=ALU.subtract,
+        )
+        dist = keep.tile([P, blocks, FREQS], F32)
+        nc.vector.scalar_tensor_tensor(
+            out=dist[:].rearrange("p b j -> p (b j)"),
+            in0=back[:].rearrange("p b j -> p (b j)"),
+            scalar=-1.0,
+            in1=back[:].rearrange("p b j -> p (b j)"),
+            op0=ALU.mult,
+            op1=ALU.max,
+        )
+        two_pi = 2.0 * math.pi
+        cos_tab = keep.tile([P, blocks, FREQS], F32)
+        sin_tab = keep.tile([P, blocks, FREQS], F32)
+        nc.scalar.activation(
+            out=cos_tab[:, 1:blocks, :], in_=dist[:, 0:TILES, :], func=ACT.Sin, scale=-two_pi, bias=math.pi / 2.0
+        )
+        nc.scalar.activation(
+            out=cos_tab[:, 0:1, :], in_=dist[:, TILES:blocks, :], func=ACT.Sin, scale=-two_pi, bias=math.pi / 2.0
+        )
+        nc.scalar.activation(out=sin_tab[:, 0:TILES, :], in_=back[:, 0:TILES, :], func=ACT.Sin, scale=-two_pi)
+        nc.scalar.activation(out=sin_tab[:, TILES:blocks, :], in_=back[:, TILES:blocks, :], func=ACT.Sin, scale=two_pi)
+
+        layer_norm_group(1)
+
+        for head in range(HEADS):
+            out_tensor = out_0 if head < HEADS_PER_OUTPUT else out_1
+            out_head = out_tensor[0, head % HEADS_PER_OUTPUT].rearrange("(p i) c -> p i c", i=TILES)
+
+            for group in range(GROUPS):
+                y = y_pool.tile([P, GROUP, CHANNELS], F32)
+                cross = cross_pool.tile([P, GROUP, ROTATED], F32)
+                for a in range(GROUP):
+                    i = group * GROUP + a
+                    tile_cols = slice(i * P, (i + 1) * P)
+                    u = acc_psum.tile([P, CHANNELS], F32)
+                    for g in range(PASSES):
+                        nc.tensor.matmul_mx(
+                            out=u[:],
+                            lhsT=x_codes[:, g, tile_cols].bitcast(FP8X4),
+                            lhsT_scale=x_scales[:, g, tile_cols],
+                            rhs=w_codes[head][:, g, :].bitcast(FP8X4),
+                            rhs_scale=w_scales[head][:, g, :],
+                            start=(g == 0),
+                            stop=(g == PASSES - 1),
+                        )
+                    nc.vector.tensor_tensor(
+                        out=y[:, a, 0:ROTATED].rearrange("p (b j d) -> p b j d", b=2, d=2),
+                        in0=u[:, 0:ROTATED].rearrange("p (b j d) -> p b j d", b=2, d=2),
+                        in1=cos_tab[:, 0 : i + 2 : i + 1, :].unsqueeze(3).to_broadcast([P, 2, FREQS, 2]),
+                        op=ALU.mult,
+                    )
+                    nc.vector.tensor_tensor(
+                        out=cross[:, a, :].rearrange("p (e j d) -> p e j d", e=2, d=2),
+                        in0=u[:, 0:ROTATED].rearrange("p (j d e) -> p e j d", d=2, e=2),
+                        in1=sin_tab[:, i : blocks : TILES - i, :].unsqueeze(3).to_broadcast([P, 2, FREQS, 2]),
+                        op=ALU.mult,
+                    )
+                    nc.scalar.copy(out=y[:, a, ROTATED:CHANNELS], in_=u[:, ROTATED:CHANNELS])
+
+                    number = head * TILES + i + W_LEAD
+                    if number < HEADS * W_PIECES:
+                        prepare_w_piece(number)
+
+                last = head == HEADS - 1 and group == GROUPS - 1
+                adder = nc.vector if last else nc.gpsimd
+                adder.tensor_tensor(
+                    out=y[:, :, 0:HALF], in0=y[:, :, 0:HALF], in1=cross[:, :, HALF:ROTATED], op=ALU.add
+                )
+                adder.tensor_tensor(
+                    out=y[:, :, HALF:ROTATED], in0=y[:, :, HALF:ROTATED], in1=cross[:, :, 0:HALF], op=ALU.add
+                )
+                nc.sync.dma_start(out=out_head[:, group * GROUP : (group + 1) * GROUP, :], in_=y[:])

@@ -31,267 +31,442 @@ K_PASS = P * PACK
 PASSES = FEATURES // K_PASS
 CHUNKS = FEATURES // P
 TILES = TOKENS // P
-GROUP = 4
-GROUPS = TILES // GROUP
-GROUP_TOKENS = GROUP * P
+PAIR = 2
+PAIRS = TILES // PAIR
+PAIR_TOKENS = PAIR * P
 BN_WIDTH = 512
 
-QUARTERS = 4
-PIECE_CHANNELS = CHANNELS // QUARTERS
-W_PIECES = PASSES * QUARTERS
-W_LEAD = W_PIECES + 2
-W_BUFS = 3
+HALVES = 2
+PIECE_CHANNELS = CHANNELS // HALVES
+W_PIECES = PASSES * HALVES
 
 ROUND_MAGIC = 12582912.0
 
+NORMALISED_ON_VECTOR = (0,)
+
 FLOPS = 2 * TOKENS * FEATURES * HEADS * CHANNELS
-
-
-def regroup(copy, grouped, planes):
-    copy(
-        out=grouped.rearrange("p (c i) t -> p c t i", i=4),
-        in_=planes.rearrange("p t (c i) -> p c t i", i=4),
-    )
 
 
 def tile_transformerencoderlayer_pa_kernel(tc, x_grid, ln_g, ln_b, w_qk, out_0, out_1):
     nc = tc.nc
     with ExitStack() as ctx:
         keep = ctx.enter_context(tc.tile_pool(name="keep", bufs=1))
-        small = ctx.enter_context(tc.tile_pool(name="small", bufs=TILES))
+        small = ctx.enter_context(tc.tile_pool(name="small", bufs=PAIRS))
         hat_pool = ctx.enter_context(tc.tile_pool(name="hat", bufs=2))
         stage = ctx.enter_context(tc.tile_pool(name="stage", bufs=2))
+        raw_pool = ctx.enter_context(tc.tile_pool(name="raw", bufs=HEADS))
         grouped_pool = ctx.enter_context(tc.tile_pool(name="grouped", bufs=2))
-        w_pool = ctx.enter_context(tc.tile_pool(name="w", bufs=W_BUFS))
-        y_pool = ctx.enter_context(tc.tile_pool(name="y", bufs=5))
-        cross_pool = ctx.enter_context(tc.tile_pool(name="cross", bufs=3))
+        w_pool = ctx.enter_context(tc.tile_pool(name="w", bufs=5))
+        y_pool = ctx.enter_context(tc.tile_pool(name="y", bufs=6))
+        cross_pool = ctx.enter_context(tc.tile_pool(name="cross", bufs=4))
         flip_psum = ctx.enter_context(tc.psum_pool(name="flip", bufs=2))
         acc_psum = ctx.enter_context(tc.psum_pool(name="acc", bufs=6))
 
+        ctx.enter_context(tc.manual_schedule())
+
+        x_sb = keep.tile([P, TILES, FEATURES], BF16)
+        x_view = x_grid[0].rearrange("(p i) d -> p i d", i=TILES)
+        w_view = w_qk.rearrange("(g p t) n -> p g t n", t=PACK, p=P)
+        w_raw = []
+
+        def load_x(pair):
+            tiles = slice(pair * PAIR, (pair + 1) * PAIR)
+            nc.sync.dma_start(out=x_sb[:, tiles, :], in_=x_view[:, tiles, :])
+
+        def load_w(head):
+            raw = raw_pool.tile([P, PASSES, PACK, CHANNELS], BF16, name="w_raw")
+            for g in range(PASSES):
+                nc.sync.dma_start(out=raw[:, g], in_=w_view[:, g, :, head * CHANNELS : (head + 1) * CHANNELS])
+            w_raw.append(raw)
+
+        load_x(0)
         gain_raw = keep.tile([P, PASSES, PACK], BF16)
         bias_raw = keep.tile([P, PASSES, PACK], BF16)
         nc.sync.dma_start(out=gain_raw[:], in_=ln_g.rearrange("(g p t) -> p g t", p=P, t=PACK))
         nc.sync.dma_start(out=bias_raw[:], in_=ln_b.rearrange("(g p t) -> p g t", p=P, t=PACK))
-
-        x_sb = keep.tile([P, TILES, FEATURES], BF16)
-        x_view = x_grid[0].rearrange("(p i) d -> p i d", i=TILES)
-
-        def load_x(group):
-            for pair in range(group * GROUP, (group + 1) * GROUP, 2):
-                nc.sync.dma_start(out=x_sb[:, pair : pair + 2, :], in_=x_view[:, pair : pair + 2, :])
-
-        w_view = w_qk.rearrange("(g p t) n -> p g t n", t=PACK, p=P)
-
-        w_raw = {}
-
-        def load_w(head):
-            w_raw[head] = w_pool.tile([P, PASSES, PACK, CHANNELS], BF16, name="w_raw")
-            for g in range(PASSES):
-                nc.sync.dma_start(
-                    out=w_raw[head][:, g], in_=w_view[:, g, :, head * CHANNELS : (head + 1) * CHANNELS]
-                )
-
-        load_x(0)
-        load_w(0)
         load_x(1)
-        for head in range(1, W_BUFS):
+        load_w(0)
+        load_x(2)
+        load_w(1)
+        load_x(3)
+        for head in range(2, HEADS):
             load_w(head)
 
         token = keep.tile([P, TILES], I32)
         nc.gpsimd.iota(token[:], pattern=[[1, TILES]], base=0, channel_multiplier=TILES)
-
         freq = keep.tile([P, P], F32)
+        nc.vector.memset(freq[:, 0:1], 1.0)
+
         ratio = (MAX_FREQ / 2.0) ** (1.0 / (FREQS - 1))
-        nc.vector.memset(freq[:, 0:1], 0.5)
         for doubling in range(7):
             filled = 2**doubling
-            nc.vector.tensor_scalar_mul(
-                out=freq[:, filled : 2 * filled], in0=freq[:, 0:filled], scalar1=ratio**filled
+            nc.gpsimd.tensor_scalar(
+                out=freq[:, filled : 2 * filled],
+                in0=freq[:, 0:filled],
+                scalar1=ratio**filled,
+                scalar2=0.0,
+                op0=ALU.mult,
+                op1=ALU.add,
             )
-
-        minus_half = keep.tile([P, 1], F32)
+        minus_half = keep.tile([P, PAIR], F32)
         nc.gpsimd.memset(minus_half[:], -0.5)
         ident = keep.tile([P, P], F32)
         make_identity(nc, ident[:])
+        gain = keep.tile([P, CHUNKS], F32)
+        bias = keep.tile([P, CHUNKS], F32)
 
-        gain_bias = keep.tile([P, 2 * CHUNKS], F32)
-        nc.vector.tensor_copy(out=gain_bias[:, 0:CHUNKS], in_=gain_raw[:].rearrange("p g t -> p (g t)"))
-        nc.vector.tensor_copy(out=gain_bias[:, CHUNKS : 2 * CHUNKS], in_=bias_raw[:].rearrange("p g t -> p (g t)"))
+        blocks = TILES + 1
+        grid_index = keep.tile([P, blocks], I32)
+        nc.vector.tensor_single_scalar(
+            out=grid_index[:, 0:1], in_=token[:, 0:1], scalar=5, op=ALU.arith_shift_right
+        )
+        nc.vector.tensor_single_scalar(out=grid_index[:, 1:blocks], in_=token[:], scalar=GRID - 1, op=ALU.bitwise_and)
+        coord = keep.tile([P, blocks], F32)
+        nc.vector.tensor_scalar(
+            out=coord[:, 0:1], in0=grid_index[:, 0:1], scalar1=-1.0 / (GRID - 1), scalar2=0.5, op0=ALU.mult, op1=ALU.add
+        )
+        nc.vector.tensor_scalar(
+            out=coord[:, 1:blocks],
+            in0=grid_index[:, 1:blocks],
+            scalar1=1.0 / (GRID - 1),
+            scalar2=-0.5,
+            op0=ALU.mult,
+            op1=ALU.add,
+        )
+        turn = keep.tile([P, blocks, FREQS], F32)
+        rounded = keep.tile([P, blocks, FREQS], F32)
+        back = keep.tile([P, blocks, FREQS], F32)
+        dist = keep.tile([P, blocks, FREQS], F32)
+        cos_tab = keep.tile([P, blocks, FREQS], F32)
+        sin_tab = keep.tile([P, blocks, FREQS], F32)
 
-        xn_t = keep.tile([P, CHUNKS, TOKENS], BF16)
-        x_codes = keep.tile([P, PASSES, TOKENS], U32, align_bytes=64)
-        x_scales = keep.tile([P, PASSES, TOKENS], U8, align_bytes=64)
+        def fold_angles(part):
+            count = part.stop - part.start
+            nc.vector.tensor_tensor(
+                out=turn[:, part],
+                in0=freq[:, 0:FREQS].unsqueeze(1).to_broadcast([P, count, FREQS]),
+                in1=coord[:, part].unsqueeze(2).to_broadcast([P, count, FREQS]),
+                op=ALU.mult,
+            )
+            nc.vector.tensor_scalar_add(out=rounded[:, part], in0=turn[:, part], scalar1=ROUND_MAGIC)
+            nc.vector.scalar_tensor_tensor(
+                out=back[:, part].rearrange("p b j -> p (b j)"),
+                in0=rounded[:, part].rearrange("p b j -> p (b j)"),
+                scalar=ROUND_MAGIC,
+                in1=turn[:, part].rearrange("p b j -> p (b j)"),
+                op0=ALU.subtract,
+                op1=ALU.subtract,
+            )
 
-        def layer_norm_group(group):
-            group_cols = slice(group * GROUP_TOKENS, (group + 1) * GROUP_TOKENS)
-            x_hat = hat_pool.tile([P, GROUP, PASSES, PACK, P], F32)
-            for a in range(GROUP):
-                x_tile = x_sb[:, group * GROUP + a, :]
-                stats = small.tile([P, FEATURES // BN_WIDTH, 6], F32)
-                for part in range(FEATURES // BN_WIDTH):
-                    nc.vector.bn_stats(out=stats[:, part, :], in_=x_tile[:, part * BN_WIDTH : (part + 1) * BN_WIDTH])
-                mean_var = small.tile([P, 2], F32)
-                nc.vector.bn_aggr(out=mean_var[:], in_=stats[:].rearrange("p a s -> p (a s)"))
-                neg_mean = small.tile([P, 1], F32)
-                nc.vector.tensor_scalar_mul(out=neg_mean[:], in0=mean_var[:, 0:1], scalar1=-1.0)
-                var_eps = small.tile([P, 1], F32)
-                nc.vector.tensor_scalar_add(out=var_eps[:], in0=mean_var[:, 1:2], scalar1=EPS)
-                rstd = small.tile([P, 1], F32)
-                nc.gpsimd.tensor_tensor(out=rstd[:], in0=var_eps[:], in1=minus_half[:], op=ALU.pow)
-                nc.vector.tensor_scalar(
-                    out=x_hat[:, a],
-                    in0=x_tile.rearrange("m (g p t) -> m g t p", g=PASSES, t=PACK),
-                    scalar1=neg_mean[:],
-                    scalar2=rstd[:],
-                    op0=ALU.add,
-                    op1=ALU.mult,
+        def make_tables(part):
+            two_pi = 2.0 * math.pi
+            nc.scalar.activation(out=sin_tab[:, part], in_=back[:, part], func=ACT.Sin, scale=-two_pi)
+            nc.scalar.activation(out=dist[:, part], in_=back[:, part], func=ACT.Abs)
+            nc.scalar.activation(
+                out=cos_tab[:, part], in_=dist[:, part], func=ACT.Sin, scale=-two_pi, bias=math.pi / 2.0
+            )
+
+        x_codes = keep.tile([P, PAIRS, PASSES, PAIR_TOKENS], U32, align_bytes=64)
+        x_scales = keep.tile([P, PAIRS, PASSES, PAIR_TOKENS], U8, align_bytes=64)
+        x_hat = {}
+
+        def load_gain_and_bias():
+            nc.gpsimd.tensor_copy(out=gain[:], in_=gain_raw[:].rearrange("p g t -> p (g t)"))
+            nc.gpsimd.tensor_copy(out=bias[:], in_=bias_raw[:].rearrange("p g t -> p (g t)"))
+
+        mean_var = {}
+        rstd = {}
+        shift = {}
+
+        def shift_of(pair):
+            shift[pair] = small.tile([P, PAIR], F32, name="shift")
+            nc.vector.scalar_tensor_tensor(
+                out=shift[pair][:],
+                in0=mean_var[pair][:, :, 0],
+                scalar=-1.0,
+                in1=rstd[pair][:],
+                op0=ALU.mult,
+                op1=ALU.mult,
+            )
+
+        def statistics(i):
+            pair, a = divmod(i, PAIR)
+            if a == 0:
+                mean_var[pair] = small.tile([P, PAIR, 2], F32, name="mean_var")
+            stats = small.tile([P, FEATURES // BN_WIDTH, 6], F32)
+            for part in range(FEATURES // BN_WIDTH):
+                nc.vector.bn_stats(
+                    out=stats[:, part, :], in_=x_sb[:, i, part * BN_WIDTH : (part + 1) * BN_WIDTH]
                 )
+            nc.vector.bn_aggr(out=mean_var[pair][:, a, :], in_=stats[:].rearrange("p a s -> p (a s)"))
+            if a == PAIR - 1:
+                scale_of(pair)
 
-            for c in range(CHUNKS):
-                flipped = flip_psum.tile([P, GROUP, P], F32, tag="flipped")
-                for a in range(GROUP):
-                    nc.tensor.transpose(flipped[:, a, :], x_hat[:, a, c // PACK, c % PACK, :], ident[:])
-                nc.scalar.activation(
-                    out=xn_t[:, c, group_cols],
-                    in_=flipped[:].rearrange("p a m -> p (a m)"),
-                    func=ACT.Identity,
-                    scale=gain_bias[:, c : c + 1],
-                    bias=gain_bias[:, CHUNKS + c : CHUNKS + c + 1],
-                )
+        def scale_of(pair):
+            var_eps = small.tile([P, PAIR], F32)
+            nc.vector.tensor_scalar_add(out=var_eps[:], in0=mean_var[pair][:, :, 1], scalar1=EPS)
+            rstd[pair] = small.tile([P, PAIR], F32, name="rstd")
+            nc.gpsimd.tensor_tensor(out=rstd[pair][:], in0=var_eps[:], in1=minus_half[:], op=ALU.pow)
 
-            for g in range(PASSES):
-                xn_grouped = stage.tile([P, GROUP_TOKENS, PACK], BF16, align_bytes=64)
-                regroup(nc.vector.tensor_copy, xn_grouped[:], xn_t[:, g * PACK : (g + 1) * PACK, group_cols])
-                nc.vector.quantize_mx(
-                    out=x_codes[:, g, group_cols].bitcast(FP8X4),
-                    scales=x_scales[:, g, group_cols],
-                    in_=xn_grouped[:].rearrange("p c t -> p (c t)"),
-                )
+        def normalise(pair):
+            x_hat[pair] = hat_pool.tile([P, PAIR, PASSES, PACK, P], F32, name="x_hat")
+            for a in range(PAIR):
+                features = x_sb[:, pair * PAIR + a, :].rearrange("m (g p t) -> m g t p", g=PASSES, t=PACK)
+                if pair in NORMALISED_ON_VECTOR:
+                    nc.vector.tensor_scalar(
+                        out=x_hat[pair][:, a],
+                        in0=features,
+                        scalar1=mean_var[pair][:, a, 0:1],
+                        scalar2=rstd[pair][:, a : a + 1],
+                        op0=ALU.subtract,
+                        op1=ALU.mult,
+                    )
+                else:
+                    nc.scalar.activation(
+                        out=x_hat[pair][:, a],
+                        in_=features,
+                        func=ACT.Identity,
+                        scale=rstd[pair][:, a : a + 1],
+                        bias=shift[pair][:, a : a + 1],
+                    )
+
+        xn_t = {}
+
+        def flip(pair):
+            xn_t[pair] = stage.tile([P, CHUNKS, PAIR_TOKENS], BF16, name="xn_t")
+            for c in range(0, CHUNKS, 2):
+                flipped = flip_psum.tile([P, 2, PAIR, P], F32)
+                for b in range(2):
+                    for a in range(PAIR):
+                        nc.tensor.transpose(
+                            flipped[:, b, a, :], x_hat[pair][:, a, (c + b) // PACK, (c + b) % PACK, :], ident[:]
+                        )
+                for b in range(2):
+                    nc.scalar.activation(
+                        out=xn_t[pair][:, c + b, :],
+                        in_=flipped[:, b].rearrange("p a m -> p (a m)"),
+                        func=ACT.Identity,
+                        scale=gain[:, c + b : c + b + 1],
+                        bias=bias[:, c + b : c + b + 1],
+                    )
+
+        def pack(pair):
+            xn_grouped = stage.tile([P, PASSES, PAIR_TOKENS, PACK], BF16, align_bytes=64)
+            nc.vector.tensor_copy(
+                out=xn_grouped[:].rearrange("p g (c i) t -> p g c t i", i=4),
+                in_=xn_t[pair][:].rearrange("p (g t) (c i) -> p g c t i", t=PACK, i=4),
+            )
+            nc.vector.quantize_mx(
+                out=x_codes[:, pair].rearrange("p g m -> p (g m)").bitcast(FP8X4),
+                scales=x_scales[:, pair].rearrange("p g m -> p (g m)"),
+                in_=xn_grouped[:].rearrange("p g m t -> p (g m t)"),
+            )
 
         w_grouped = {}
         w_codes = {}
         w_scales = {}
 
-        def prepare_w_piece(number):
+        def prepare_w_piece(number, copy):
             head, piece = divmod(number, W_PIECES)
-            g, quarter = divmod(piece, QUARTERS)
-            piece_cols = slice(quarter * PIECE_CHANNELS, (quarter + 1) * PIECE_CHANNELS)
+            g, half = divmod(piece, HALVES)
+            cols = slice(half * PIECE_CHANNELS, (half + 1) * PIECE_CHANNELS)
             if piece == 0:
                 w_grouped[head] = grouped_pool.tile(
                     [P, PASSES, CHANNELS, PACK], BF16, align_bytes=64, name="w_grouped"
                 )
-            regroup(nc.scalar.copy, w_grouped[head][:, g, piece_cols, :], w_raw[head][:, g, :, piece_cols])
-            if piece == W_PIECES - 1:
-                w_codes[head] = w_pool.tile([P, PASSES, CHANNELS], U32, align_bytes=64, name="w_codes")
-                w_scales[head] = w_pool.tile([P, PASSES, CHANNELS], U8, align_bytes=64, name="w_scales")
-                nc.vector.quantize_mx(
-                    out=w_codes[head][:].rearrange("p g c -> p (g c)").bitcast(FP8X4),
-                    scales=w_scales[head][:].rearrange("p g c -> p (g c)"),
-                    in_=w_grouped[head][:].rearrange("p g c t -> p (g c t)"),
+            copy(
+                out=w_grouped[head][:, g, cols, :].rearrange("p (c i) t -> p c t i", i=4),
+                in_=w_raw[head][:, g, :, cols].rearrange("p t (c i) -> p c t i", i=4),
+            )
+
+        def quantise_w(head):
+            w_codes[head] = w_pool.tile([P, PASSES, CHANNELS], U32, align_bytes=64, name="w_codes")
+            w_scales[head] = w_pool.tile([P, PASSES, CHANNELS], U8, align_bytes=64, name="w_scales")
+            nc.vector.quantize_mx(
+                out=w_codes[head][:].rearrange("p g c -> p (g c)").bitcast(FP8X4),
+                scales=w_scales[head][:].rearrange("p g c -> p (g c)"),
+                in_=w_grouped[head][:].rearrange("p g c t -> p (g c t)"),
+            )
+
+        u = {}
+
+        def project(head, pair):
+            for a in range(PAIR):
+                tile_cols = slice(a * P, (a + 1) * P)
+                acc = acc_psum.tile([P, CHANNELS], F32)
+                for g in range(PASSES):
+                    nc.tensor.matmul_mx(
+                        out=acc[:],
+                        lhsT=x_codes[:, pair, g, tile_cols].bitcast(FP8X4),
+                        lhsT_scale=x_scales[:, pair, g, tile_cols],
+                        rhs=w_codes[head][:, g, :].bitcast(FP8X4),
+                        rhs_scale=w_scales[head][:, g, :],
+                        start=(g == 0),
+                        stop=(g == PASSES - 1),
+                    )
+                u[head, pair * PAIR + a] = acc
+
+        y = {}
+        crosses = {}
+
+        def pass_through(head, pair):
+            for a in range(PAIR):
+                nc.scalar.copy(
+                    out=y[head, pair][:, a, ROTATED:CHANNELS], in_=u[head, pair * PAIR + a][:, ROTATED:CHANNELS]
                 )
-                if head + W_BUFS < HEADS:
-                    load_w(head + W_BUFS)
 
-        layer_norm_group(0)
-        for number in range(W_LEAD):
-            prepare_w_piece(number)
+        def rotate(head, pair, last):
+            y_pair = y_pool.tile([P, PAIR, CHANNELS], F32)
+            y[head, pair] = y_pair
+            cross = cross_pool.tile([P, PAIR, ROTATED], F32)
+            for a in range(PAIR):
+                i = pair * PAIR + a
+                cos_in = cos_tab[:, 0 : i + 2 : i + 1, :].unsqueeze(3).to_broadcast([P, 2, FREQS, 2])
+                sin_in = sin_tab[:, 0 : i + 2 : i + 1, :].unsqueeze(3).to_broadcast([P, 2, FREQS, 2])
+                nc.vector.tensor_tensor(
+                    out=y_pair[:, a, 0:ROTATED].rearrange("p (b j d) -> p b j d", b=2, d=2),
+                    in0=u[head, i][:, 0:ROTATED].rearrange("p (b j d) -> p b j d", b=2, d=2),
+                    in1=cos_in,
+                    op=ALU.mult,
+                )
+                nc.vector.tensor_tensor(
+                    out=cross[:, a, :].rearrange("p (b j d) -> p b j d", b=2, d=2),
+                    in0=u[head, i][:, 0:ROTATED].rearrange("p (j d e) -> p e j d", d=2, e=2)[:, ::-1],
+                    in1=sin_in,
+                    op=ALU.mult,
+                )
+                if last:
+                    nc.vector.tensor_tensor(
+                        out=y_pair[:, a, 0:ROTATED], in0=y_pair[:, a, 0:ROTATED], in1=cross[:, a, :], op=ALU.add
+                    )
+            crosses[head, pair] = cross
 
-        blocks = TILES + 1
-        grid_index = keep.tile([P, blocks], I32)
-        nc.vector.tensor_single_scalar(out=grid_index[:, 0:TILES], in_=token[:], scalar=GRID - 1, op=ALU.bitwise_and)
-        nc.vector.tensor_single_scalar(
-            out=grid_index[:, TILES:blocks], in_=token[:, 0:1], scalar=5, op=ALU.arith_shift_right
-        )
-        coord = keep.tile([P, blocks], F32)
-        nc.vector.tensor_scalar(
-            out=coord[:], in0=grid_index[:], scalar1=2.0 / (GRID - 1), scalar2=-1.0, op0=ALU.mult, op1=ALU.add
-        )
-        turn = keep.tile([P, blocks, FREQS], F32)
-        nc.vector.tensor_tensor(
-            out=turn[:],
-            in0=freq[:, 0:FREQS].unsqueeze(1).to_broadcast([P, blocks, FREQS]),
-            in1=coord[:].unsqueeze(2).to_broadcast([P, blocks, FREQS]),
-            op=ALU.mult,
-        )
-        rounded = keep.tile([P, blocks, FREQS], F32)
-        nc.vector.tensor_scalar_add(out=rounded[:], in0=turn[:], scalar1=ROUND_MAGIC)
-        back = keep.tile([P, blocks, FREQS], F32)
-        nc.vector.scalar_tensor_tensor(
-            out=back[:].rearrange("p b j -> p (b j)"),
-            in0=rounded[:].rearrange("p b j -> p (b j)"),
-            scalar=ROUND_MAGIC,
-            in1=turn[:].rearrange("p b j -> p (b j)"),
-            op0=ALU.subtract,
-            op1=ALU.subtract,
-        )
-        dist = keep.tile([P, blocks, FREQS], F32)
-        nc.vector.scalar_tensor_tensor(
-            out=dist[:].rearrange("p b j -> p (b j)"),
-            in0=back[:].rearrange("p b j -> p (b j)"),
-            scalar=-1.0,
-            in1=back[:].rearrange("p b j -> p (b j)"),
-            op0=ALU.mult,
-            op1=ALU.max,
-        )
-        two_pi = 2.0 * math.pi
-        cos_tab = keep.tile([P, blocks, FREQS], F32)
-        sin_tab = keep.tile([P, blocks, FREQS], F32)
-        nc.scalar.activation(
-            out=cos_tab[:, 1:blocks, :], in_=dist[:, 0:TILES, :], func=ACT.Sin, scale=-two_pi, bias=math.pi / 2.0
-        )
-        nc.scalar.activation(
-            out=cos_tab[:, 0:1, :], in_=dist[:, TILES:blocks, :], func=ACT.Sin, scale=-two_pi, bias=math.pi / 2.0
-        )
-        nc.scalar.activation(out=sin_tab[:, 0:TILES, :], in_=back[:, 0:TILES, :], func=ACT.Sin, scale=-two_pi)
-        nc.scalar.activation(out=sin_tab[:, TILES:blocks, :], in_=back[:, TILES:blocks, :], func=ACT.Sin, scale=two_pi)
+        def add_cross(head, pair):
+            y_pair = y[head, pair]
+            nc.gpsimd.tensor_tensor(
+                out=y_pair[:, :, 0:ROTATED], in0=y_pair[:, :, 0:ROTATED], in1=crosses[head, pair][:], op=ALU.add
+            )
 
-        layer_norm_group(1)
-
-        for head in range(HEADS):
+        def store(head, pair, last):
             out_tensor = out_0 if head < HEADS_PER_OUTPUT else out_1
             out_head = out_tensor[0, head % HEADS_PER_OUTPUT].rearrange("(p i) c -> p i c", i=TILES)
+            for first in range(0, PAIR, 1 if last else PAIR):
+                count = 1 if last else PAIR
+                tiles = slice(pair * PAIR + first, pair * PAIR + first + count)
+                nc.sync.dma_start(out=out_head[:, tiles, :], in_=y[head, pair][:, first : first + count, :])
 
-            for group in range(GROUPS):
-                y = y_pool.tile([P, GROUP, CHANNELS], F32)
-                cross = cross_pool.tile([P, GROUP, ROTATED], F32)
-                for a in range(GROUP):
-                    i = group * GROUP + a
-                    tile_cols = slice(i * P, (i + 1) * P)
-                    u = acc_psum.tile([P, CHANNELS], F32)
-                    for g in range(PASSES):
-                        nc.tensor.matmul_mx(
-                            out=u[:],
-                            lhsT=x_codes[:, g, tile_cols].bitcast(FP8X4),
-                            lhsT_scale=x_scales[:, g, tile_cols],
-                            rhs=w_codes[head][:, g, :].bitcast(FP8X4),
-                            rhs_scale=w_scales[head][:, g, :],
-                            start=(g == 0),
-                            stop=(g == PASSES - 1),
-                        )
-                    nc.vector.tensor_tensor(
-                        out=y[:, a, 0:ROTATED].rearrange("p (b j d) -> p b j d", b=2, d=2),
-                        in0=u[:, 0:ROTATED].rearrange("p (b j d) -> p b j d", b=2, d=2),
-                        in1=cos_tab[:, 0 : i + 2 : i + 1, :].unsqueeze(3).to_broadcast([P, 2, FREQS, 2]),
-                        op=ALU.mult,
-                    )
-                    nc.vector.tensor_tensor(
-                        out=cross[:, a, :].rearrange("p (e j d) -> p e j d", e=2, d=2),
-                        in0=u[:, 0:ROTATED].rearrange("p (j d e) -> p e j d", d=2, e=2),
-                        in1=sin_tab[:, i : blocks : TILES - i, :].unsqueeze(3).to_broadcast([P, 2, FREQS, 2]),
-                        op=ALU.mult,
-                    )
-                    nc.scalar.copy(out=y[:, a, ROTATED:CHANNELS], in_=u[:, ROTATED:CHANNELS])
-
-                    number = head * TILES + i + W_LEAD
-                    if number < HEADS * W_PIECES:
-                        prepare_w_piece(number)
-
-                last = head == HEADS - 1 and group == GROUPS - 1
-                adder = nc.vector if last else nc.gpsimd
-                adder.tensor_tensor(
-                    out=y[:, :, 0:HALF], in0=y[:, :, 0:HALF], in1=cross[:, :, HALF:ROTATED], op=ALU.add
-                )
-                adder.tensor_tensor(
-                    out=y[:, :, HALF:ROTATED], in0=y[:, :, HALF:ROTATED], in1=cross[:, :, 0:HALF], op=ALU.add
-                )
-                nc.sync.dma_start(out=out_head[:, group * GROUP : (group + 1) * GROUP, :], in_=y[:])
+        first_blocks = slice(0, 1 + PAIR)
+        other_blocks = slice(1 + PAIR, blocks)
+        fold_angles(first_blocks)
+        make_tables(first_blocks)
+        statistics(0)
+        statistics(1)
+        load_gain_and_bias()
+        fold_angles(other_blocks)
+        prepare_w_piece(0, nc.scalar.copy)
+        make_tables(other_blocks)
+        prepare_w_piece(2, nc.scalar.copy)
+        normalise(0)
+        flip(0)
+        statistics(2)
+        statistics(3)
+        prepare_w_piece(1, nc.vector.tensor_copy)
+        prepare_w_piece(3, nc.vector.tensor_copy)
+        shift_of(1)
+        quantise_w(0)
+        pack(0)
+        project(0, 0)
+        prepare_w_piece(4, nc.scalar.copy)
+        prepare_w_piece(5, nc.scalar.copy)
+        normalise(1)
+        prepare_w_piece(6, nc.scalar.copy)
+        prepare_w_piece(7, nc.scalar.copy)
+        statistics(4)
+        rotate(0, 0, False)
+        add_cross(0, 0)
+        flip(1)
+        statistics(5)
+        quantise_w(1)
+        project(1, 0)
+        statistics(6)
+        shift_of(2)
+        pass_through(0, 0)
+        store(0, 0, False)
+        pack(1)
+        project(0, 1)
+        prepare_w_piece(8, nc.scalar.copy)
+        rotate(1, 0, False)
+        add_cross(1, 0)
+        project(1, 1)
+        prepare_w_piece(9, nc.scalar.copy)
+        prepare_w_piece(10, nc.scalar.copy)
+        prepare_w_piece(11, nc.scalar.copy)
+        normalise(2)
+        pass_through(1, 0)
+        store(1, 0, False)
+        statistics(7)
+        rotate(0, 1, False)
+        add_cross(0, 1)
+        flip(2)
+        pass_through(0, 1)
+        store(0, 1, False)
+        rotate(1, 1, False)
+        add_cross(1, 1)
+        shift_of(3)
+        quantise_w(2)
+        project(2, 0)
+        pass_through(1, 1)
+        store(1, 1, False)
+        prepare_w_piece(12, nc.scalar.copy)
+        prepare_w_piece(13, nc.scalar.copy)
+        pack(2)
+        project(2, 1)
+        rotate(2, 0, False)
+        add_cross(2, 0)
+        prepare_w_piece(14, nc.scalar.copy)
+        prepare_w_piece(15, nc.scalar.copy)
+        project(0, 2)
+        normalise(3)
+        pass_through(2, 0)
+        store(2, 0, False)
+        rotate(2, 1, False)
+        add_cross(2, 1)
+        flip(3)
+        project(1, 2)
+        pass_through(2, 1)
+        store(2, 1, False)
+        rotate(0, 2, False)
+        add_cross(0, 2)
+        quantise_w(3)
+        project(2, 2)
+        rotate(1, 2, False)
+        add_cross(1, 2)
+        pass_through(0, 2)
+        store(0, 2, False)
+        pass_through(1, 2)
+        store(1, 2, False)
+        prepare_w_piece(16, nc.scalar.copy)
+        pack(3)
+        project(3, 0)
+        rotate(2, 2, False)
+        add_cross(2, 2)
+        project(3, 1)
+        pass_through(2, 2)
+        store(2, 2, False)
+        prepare_w_piece(17, nc.scalar.copy)
+        steps = [(3, 0), (3, 1), (3, 2), (0, 3), (1, 3), (2, 3), (3, 3)] + [(head, pair) for head in range(4, HEADS) for pair in range(PAIRS)]
+        piece = 4 * W_PIECES + 2
+        for step in range(0, len(steps)):
+            last = step == len(steps) - 1
+            if not last and step > 0:
+                project(*steps[step + 1])
+            if piece < HEADS * W_PIECES:
+                prepare_w_piece(piece, nc.scalar.copy)
+            rotate(*steps[step], last)
+            pass_through(*steps[step])
+            if not last:
+                add_cross(*steps[step])
+            store(*steps[step], last)
+            piece += 1
+            if piece % W_PIECES == 0 and piece <= HEADS * W_PIECES:
+                quantise_w(piece // W_PIECES - 1)

@@ -56,7 +56,7 @@ def tile_transformerencoderlayer_pa_kernel(tc, x_grid, ln_g, ln_b, w_qk, out_0, 
         stage = ctx.enter_context(tc.tile_pool(name="stage", bufs=2))
         raw_pool = ctx.enter_context(tc.tile_pool(name="raw", bufs=HEADS))
         grouped_pool = ctx.enter_context(tc.tile_pool(name="grouped", bufs=2))
-        w_pool = ctx.enter_context(tc.tile_pool(name="w", bufs=5))
+        w_pool = ctx.enter_context(tc.tile_pool(name="w", bufs=6))
         y_pool = ctx.enter_context(tc.tile_pool(name="y", bufs=6))
         cross_pool = ctx.enter_context(tc.tile_pool(name="cross", bufs=4))
         flip_psum = ctx.enter_context(tc.psum_pool(name="flip", bufs=2))
@@ -84,30 +84,36 @@ def tile_transformerencoderlayer_pa_kernel(tc, x_grid, ln_g, ln_b, w_qk, out_0, 
         bias_raw = keep.tile([P, PASSES, PACK], BF16)
         nc.sync.dma_start(out=gain_raw[:], in_=ln_g.rearrange("(g p t) -> p g t", p=P, t=PACK))
         nc.sync.dma_start(out=bias_raw[:], in_=ln_b.rearrange("(g p t) -> p g t", p=P, t=PACK))
-        load_x(1)
         load_w(0)
-        load_x(2)
+        load_x(1)
         load_w(1)
+        load_x(2)
         load_x(3)
         for head in range(2, HEADS):
             load_w(head)
 
         token = keep.tile([P, TILES], I32)
         nc.gpsimd.iota(token[:], pattern=[[1, TILES]], base=0, channel_multiplier=TILES)
-        freq = keep.tile([P, P], F32)
-        nc.vector.memset(freq[:, 0:1], 1.0)
 
         ratio = (MAX_FREQ / 2.0) ** (1.0 / (FREQS - 1))
-        for doubling in range(7):
+        coarse = keep.tile([P, 16], F32)
+        fine = keep.tile([P, 16], F32)
+        nc.gpsimd.memset(coarse[:, 0:1], 1.0)
+        nc.vector.memset(fine[:, 0:1], 1.0)
+        for doubling in range(4):
             filled = 2**doubling
             nc.gpsimd.tensor_scalar(
-                out=freq[:, filled : 2 * filled],
-                in0=freq[:, 0:filled],
-                scalar1=ratio**filled,
+                out=coarse[:, filled : 2 * filled],
+                in0=coarse[:, 0:filled],
+                scalar1=ratio ** (10 * filled),
                 scalar2=0.0,
                 op0=ALU.mult,
                 op1=ALU.add,
             )
+            nc.vector.tensor_scalar_mul(
+                out=fine[:, filled : 2 * filled], in0=fine[:, 0:filled], scalar1=ratio**filled
+            )
+        freq = keep.tile([P, FREQS], F32)
         minus_half = keep.tile([P, PAIR], F32)
         nc.gpsimd.memset(minus_half[:], -0.5)
         ident = keep.tile([P, P], F32)
@@ -133,6 +139,12 @@ def tile_transformerencoderlayer_pa_kernel(tc, x_grid, ln_g, ln_b, w_qk, out_0, 
             op0=ALU.mult,
             op1=ALU.add,
         )
+        nc.vector.tensor_tensor(
+            out=freq[:].rearrange("p (a b) -> p a b", b=10),
+            in0=coarse[:, 0:10].unsqueeze(2).to_broadcast([P, 10, 10]),
+            in1=fine[:, 0:10].unsqueeze(1).to_broadcast([P, 10, 10]),
+            op=ALU.mult,
+        )
         turn = keep.tile([P, blocks, FREQS], F32)
         rounded = keep.tile([P, blocks, FREQS], F32)
         back = keep.tile([P, blocks, FREQS], F32)
@@ -144,7 +156,7 @@ def tile_transformerencoderlayer_pa_kernel(tc, x_grid, ln_g, ln_b, w_qk, out_0, 
             count = part.stop - part.start
             nc.vector.tensor_tensor(
                 out=turn[:, part],
-                in0=freq[:, 0:FREQS].unsqueeze(1).to_broadcast([P, count, FREQS]),
+                in0=freq[:].unsqueeze(1).to_broadcast([P, count, FREQS]),
                 in1=coord[:, part].unsqueeze(2).to_broadcast([P, count, FREQS]),
                 op=ALU.mult,
             )
@@ -178,17 +190,6 @@ def tile_transformerencoderlayer_pa_kernel(tc, x_grid, ln_g, ln_b, w_qk, out_0, 
         rstd = {}
         shift = {}
 
-        def shift_of(pair):
-            shift[pair] = small.tile([P, PAIR], F32, name="shift")
-            nc.vector.scalar_tensor_tensor(
-                out=shift[pair][:],
-                in0=mean_var[pair][:, :, 0],
-                scalar=-1.0,
-                in1=rstd[pair][:],
-                op0=ALU.mult,
-                op1=ALU.mult,
-            )
-
         def statistics(i):
             pair, a = divmod(i, PAIR)
             if a == 0:
@@ -204,9 +205,18 @@ def tile_transformerencoderlayer_pa_kernel(tc, x_grid, ln_g, ln_b, w_qk, out_0, 
 
         def scale_of(pair):
             var_eps = small.tile([P, PAIR], F32)
-            nc.vector.tensor_scalar_add(out=var_eps[:], in0=mean_var[pair][:, :, 1], scalar1=EPS)
+            nc.gpsimd.tensor_scalar(
+                out=var_eps[:], in0=mean_var[pair][:, :, 1], scalar1=1.0, scalar2=EPS, op0=ALU.mult, op1=ALU.add
+            )
             rstd[pair] = small.tile([P, PAIR], F32, name="rstd")
             nc.gpsimd.tensor_tensor(out=rstd[pair][:], in0=var_eps[:], in1=minus_half[:], op=ALU.pow)
+            if pair not in NORMALISED_ON_VECTOR:
+                minus_mean = small.tile([P, PAIR], F32)
+                nc.gpsimd.tensor_scalar(
+                    out=minus_mean[:], in0=mean_var[pair][:, :, 0], scalar1=-1.0, scalar2=0.0, op0=ALU.mult, op1=ALU.add
+                )
+                shift[pair] = small.tile([P, PAIR], F32, name="shift")
+                nc.gpsimd.tensor_tensor(out=shift[pair][:], in0=minus_mean[:], in1=rstd[pair][:], op=ALU.mult)
 
         def normalise(pair):
             x_hat[pair] = hat_pool.tile([P, PAIR, PASSES, PACK, P], F32, name="x_hat")
@@ -235,7 +245,7 @@ def tile_transformerencoderlayer_pa_kernel(tc, x_grid, ln_g, ln_b, w_qk, out_0, 
         def flip(pair):
             xn_t[pair] = stage.tile([P, CHUNKS, PAIR_TOKENS], BF16, name="xn_t")
             for c in range(0, CHUNKS, 2):
-                flipped = flip_psum.tile([P, 2, PAIR, P], F32)
+                flipped = flip_psum.tile([P, 2, PAIR, P], F32, tag="flipped")
                 for b in range(2):
                     for a in range(PAIR):
                         nc.tensor.transpose(
@@ -251,11 +261,14 @@ def tile_transformerencoderlayer_pa_kernel(tc, x_grid, ln_g, ln_b, w_qk, out_0, 
                     )
 
         def pack(pair):
-            xn_grouped = stage.tile([P, PASSES, PAIR_TOKENS, PACK], BF16, align_bytes=64)
+            xn_grouped = stage.tile([P, PASSES, PAIR_TOKENS, PACK], BF16, align_bytes=64, name="xn_grouped")
             nc.vector.tensor_copy(
                 out=xn_grouped[:].rearrange("p g (c i) t -> p g c t i", i=4),
                 in_=xn_t[pair][:].rearrange("p (g t) (c i) -> p g c t i", t=PACK, i=4),
             )
+            quantise_x(pair, xn_grouped)
+
+        def quantise_x(pair, xn_grouped):
             nc.vector.quantize_mx(
                 out=x_codes[:, pair].rearrange("p g m -> p (g m)").bitcast(FP8X4),
                 scales=x_scales[:, pair].rearrange("p g m -> p (g m)"),
@@ -343,9 +356,13 @@ def tile_transformerencoderlayer_pa_kernel(tc, x_grid, ln_g, ln_b, w_qk, out_0, 
 
         def add_cross(head, pair):
             y_pair = y[head, pair]
-            nc.gpsimd.tensor_tensor(
-                out=y_pair[:, :, 0:ROTATED], in0=y_pair[:, :, 0:ROTATED], in1=crosses[head, pair][:], op=ALU.add
-            )
+            for a in range(PAIR):
+                nc.gpsimd.tensor_tensor(
+                    out=y_pair[:, a, 0:ROTATED],
+                    in0=y_pair[:, a, 0:ROTATED],
+                    in1=crosses[head, pair][:, a, :],
+                    op=ALU.add,
+                )
 
         def store(head, pair, last):
             out_tensor = out_0 if head < HEADS_PER_OUTPUT else out_1
@@ -372,7 +389,6 @@ def tile_transformerencoderlayer_pa_kernel(tc, x_grid, ln_g, ln_b, w_qk, out_0, 
         statistics(3)
         prepare_w_piece(1, nc.vector.tensor_copy)
         prepare_w_piece(3, nc.vector.tensor_copy)
-        shift_of(1)
         quantise_w(0)
         pack(0)
         project(0, 0)
@@ -389,7 +405,6 @@ def tile_transformerencoderlayer_pa_kernel(tc, x_grid, ln_g, ln_b, w_qk, out_0, 
         quantise_w(1)
         project(1, 0)
         statistics(6)
-        shift_of(2)
         pass_through(0, 0)
         store(0, 0, False)
         pack(1)
@@ -412,7 +427,6 @@ def tile_transformerencoderlayer_pa_kernel(tc, x_grid, ln_g, ln_b, w_qk, out_0, 
         store(0, 1, False)
         rotate(1, 1, False)
         add_cross(1, 1)
-        shift_of(3)
         quantise_w(2)
         project(2, 0)
         pass_through(1, 1)

@@ -44,6 +44,10 @@ ROUND_MAGIC = 12582912.0
 
 NORMALISED_ON_VECTOR = (0,)
 
+FIRST_LONG_HEAD = 4
+Y_BUFS = {2: 4, 4: 3}
+CROSS_BUFS = {2: 3, 4: 2}
+
 FLOPS = 2 * TOKENS * FEATURES * HEADS * CHANNELS
 
 
@@ -54,9 +58,9 @@ def tile_transformerencoderlayer_pa_kernel(tc, x_grid, ln_g, ln_b, w_qk, out_0, 
         small = ctx.enter_context(tc.tile_pool(name="small", bufs=PAIRS))
         hat_pool = ctx.enter_context(tc.tile_pool(name="hat", bufs=2))
         stage = ctx.enter_context(tc.tile_pool(name="stage", bufs=2))
-        raw_pool = ctx.enter_context(tc.tile_pool(name="raw", bufs=HEADS))
+        raw_pool = ctx.enter_context(tc.tile_pool(name="raw", bufs=6))
         grouped_pool = ctx.enter_context(tc.tile_pool(name="grouped", bufs=2))
-        w_pool = ctx.enter_context(tc.tile_pool(name="w", bufs=6))
+        w_pool = ctx.enter_context(tc.tile_pool(name="w", bufs=5))
         y_pool = ctx.enter_context(tc.tile_pool(name="y", bufs=6))
         cross_pool = ctx.enter_context(tc.tile_pool(name="cross", bufs=4))
         flip_psum = ctx.enter_context(tc.psum_pool(name="flip", bufs=2))
@@ -84,8 +88,8 @@ def tile_transformerencoderlayer_pa_kernel(tc, x_grid, ln_g, ln_b, w_qk, out_0, 
         bias_raw = keep.tile([P, PASSES, PACK], BF16)
         nc.sync.dma_start(out=gain_raw[:], in_=ln_g.rearrange("(g p t) -> p g t", p=P, t=PACK))
         nc.sync.dma_start(out=bias_raw[:], in_=ln_b.rearrange("(g p t) -> p g t", p=P, t=PACK))
-        load_w(0)
         load_x(1)
+        load_w(0)
         load_w(1)
         load_x(2)
         load_x(3)
@@ -148,7 +152,6 @@ def tile_transformerencoderlayer_pa_kernel(tc, x_grid, ln_g, ln_b, w_qk, out_0, 
         turn = keep.tile([P, blocks, FREQS], F32)
         rounded = keep.tile([P, blocks, FREQS], F32)
         back = keep.tile([P, blocks, FREQS], F32)
-        dist = keep.tile([P, blocks, FREQS], F32)
         cos_tab = keep.tile([P, blocks, FREQS], F32)
         sin_tab = keep.tile([P, blocks, FREQS], F32)
 
@@ -173,9 +176,9 @@ def tile_transformerencoderlayer_pa_kernel(tc, x_grid, ln_g, ln_b, w_qk, out_0, 
         def make_tables(part):
             two_pi = 2.0 * math.pi
             nc.scalar.activation(out=sin_tab[:, part], in_=back[:, part], func=ACT.Sin, scale=-two_pi)
-            nc.scalar.activation(out=dist[:, part], in_=back[:, part], func=ACT.Abs)
+            nc.scalar.activation(out=rounded[:, part], in_=back[:, part], func=ACT.Abs)
             nc.scalar.activation(
-                out=cos_tab[:, part], in_=dist[:, part], func=ACT.Sin, scale=-two_pi, bias=math.pi / 2.0
+                out=cos_tab[:, part], in_=rounded[:, part], func=ACT.Sin, scale=-two_pi, bias=math.pi / 2.0
             )
 
         x_codes = keep.tile([P, PAIRS, PASSES, PAIR_TOKENS], U32, align_bytes=64)
@@ -260,19 +263,21 @@ def tile_transformerencoderlayer_pa_kernel(tc, x_grid, ln_g, ln_b, w_qk, out_0, 
                         bias=bias[:, c + b : c + b + 1],
                     )
 
-        def pack(pair):
+        def pack(pair, copy):
             xn_grouped = stage.tile([P, PASSES, PAIR_TOKENS, PACK], BF16, align_bytes=64, name="xn_grouped")
-            nc.vector.tensor_copy(
+            copy(
                 out=xn_grouped[:].rearrange("p g (c i) t -> p g c t i", i=4),
                 in_=xn_t[pair][:].rearrange("p (g t) (c i) -> p g c t i", t=PACK, i=4),
             )
-            quantise_x(pair, xn_grouped)
+            grouped_x[pair] = xn_grouped
 
-        def quantise_x(pair, xn_grouped):
+        grouped_x = {}
+
+        def quantise_x(pair):
             nc.vector.quantize_mx(
                 out=x_codes[:, pair].rearrange("p g m -> p (g m)").bitcast(FP8X4),
                 scales=x_scales[:, pair].rearrange("p g m -> p (g m)"),
-                in_=xn_grouped[:].rearrange("p g m t -> p (g m t)"),
+                in_=grouped_x[pair][:].rearrange("p g m t -> p (g m t)"),
             )
 
         w_grouped = {}
@@ -303,6 +308,12 @@ def tile_transformerencoderlayer_pa_kernel(tc, x_grid, ln_g, ln_b, w_qk, out_0, 
 
         u = {}
 
+        def run_tiles(head):
+            return 2 * PAIR if head >= FIRST_LONG_HEAD else PAIR
+
+        def place(head, pair):
+            return divmod(pair, run_tiles(head) // PAIR)
+
         def project(head, pair):
             for a in range(PAIR):
                 tile_cols = slice(a * P, (a + 1) * P)
@@ -323,15 +334,20 @@ def tile_transformerencoderlayer_pa_kernel(tc, x_grid, ln_g, ln_b, w_qk, out_0, 
         crosses = {}
 
         def pass_through(head, pair):
+            run, part = place(head, pair)
             for a in range(PAIR):
                 nc.scalar.copy(
-                    out=y[head, pair][:, a, ROTATED:CHANNELS], in_=u[head, pair * PAIR + a][:, ROTATED:CHANNELS]
+                    out=y[head, run][:, part * PAIR + a, ROTATED:CHANNELS], in_=u[head, pair * PAIR + a][:, ROTATED:CHANNELS]
                 )
 
-        def rotate(head, pair, last):
-            y_pair = y_pool.tile([P, PAIR, CHANNELS], F32)
-            y[head, pair] = y_pair
-            cross = cross_pool.tile([P, PAIR, ROTATED], F32)
+        def rotate(head, pair):
+            run, part = place(head, pair)
+            if part == 0:
+                tiles = run_tiles(head)
+                y[head, run] = y_pool.tile([P, tiles, CHANNELS], F32, name="y%d" % tiles, bufs=Y_BUFS[tiles])
+                crosses[head, run] = cross_pool.tile([P, tiles, ROTATED], F32, name="cross%d" % tiles, bufs=CROSS_BUFS[tiles])
+            y_pair = y[head, run][:, part * PAIR : (part + 1) * PAIR]
+            cross = crosses[head, run][:, part * PAIR : (part + 1) * PAIR]
             for a in range(PAIR):
                 i = pair * PAIR + a
                 cos_in = cos_tab[:, 0 : i + 2 : i + 1, :].unsqueeze(3).to_broadcast([P, 2, FREQS, 2])
@@ -348,49 +364,44 @@ def tile_transformerencoderlayer_pa_kernel(tc, x_grid, ln_g, ln_b, w_qk, out_0, 
                     in1=sin_in,
                     op=ALU.mult,
                 )
-                if last:
-                    nc.vector.tensor_tensor(
-                        out=y_pair[:, a, 0:ROTATED], in0=y_pair[:, a, 0:ROTATED], in1=cross[:, a, :], op=ALU.add
-                    )
-            crosses[head, pair] = cross
 
-        def add_cross(head, pair):
-            y_pair = y[head, pair]
-            for a in range(PAIR):
-                nc.gpsimd.tensor_tensor(
-                    out=y_pair[:, a, 0:ROTATED],
-                    in0=y_pair[:, a, 0:ROTATED],
-                    in1=crosses[head, pair][:, a, :],
-                    op=ALU.add,
-                )
+        def add_cross(head, run):
+            y_run = y[head, run][:, :, 0:ROTATED]
+            nc.gpsimd.tensor_tensor(out=y_run, in0=y_run, in1=crosses[head, run][:], op=ALU.add)
 
-        def store(head, pair, last):
+        def run_slice(head, run):
             out_tensor = out_0 if head < HEADS_PER_OUTPUT else out_1
+            tiles = run_tiles(head)
             out_head = out_tensor[0, head % HEADS_PER_OUTPUT].rearrange("(p i) c -> p i c", i=TILES)
-            for first in range(0, PAIR, 1 if last else PAIR):
-                count = 1 if last else PAIR
-                tiles = slice(pair * PAIR + first, pair * PAIR + first + count)
-                nc.sync.dma_start(out=out_head[:, tiles, :], in_=y[head, pair][:, first : first + count, :])
+            return out_head[:, run * tiles : (run + 1) * tiles, :]
 
-        first_blocks = slice(0, 1 + PAIR)
-        other_blocks = slice(1 + PAIR, blocks)
-        fold_angles(first_blocks)
-        make_tables(first_blocks)
+        def store(head, run):
+            nc.sync.dma_start(out=run_slice(head, run), in_=y[head, run][:])
+
+        def add_and_store_last(head, run):
+            for a in range(run_tiles(head)):
+                y_tile = y[head, run][:, a, :]
+                nc.vector.tensor_tensor(
+                    out=y_tile[:, 0:ROTATED], in0=y_tile[:, 0:ROTATED], in1=crosses[head, run][:, a, :], op=ALU.add
+                )
+                nc.sync.dma_start(out=run_slice(head, run)[:, a, :], in_=y_tile)
+
+        fold_angles(slice(0, blocks))
+        make_tables(slice(0, blocks))
         statistics(0)
         statistics(1)
         load_gain_and_bias()
-        fold_angles(other_blocks)
         prepare_w_piece(0, nc.scalar.copy)
-        make_tables(other_blocks)
         prepare_w_piece(2, nc.scalar.copy)
+        statistics(2)
         normalise(0)
         flip(0)
-        statistics(2)
         statistics(3)
         prepare_w_piece(1, nc.vector.tensor_copy)
         prepare_w_piece(3, nc.vector.tensor_copy)
         quantise_w(0)
-        pack(0)
+        pack(0, nc.vector.tensor_copy)
+        quantise_x(0)
         project(0, 0)
         prepare_w_piece(4, nc.scalar.copy)
         prepare_w_piece(5, nc.scalar.copy)
@@ -398,7 +409,7 @@ def tile_transformerencoderlayer_pa_kernel(tc, x_grid, ln_g, ln_b, w_qk, out_0, 
         prepare_w_piece(6, nc.scalar.copy)
         prepare_w_piece(7, nc.scalar.copy)
         statistics(4)
-        rotate(0, 0, False)
+        rotate(0, 0)
         add_cross(0, 0)
         flip(1)
         statistics(5)
@@ -406,11 +417,12 @@ def tile_transformerencoderlayer_pa_kernel(tc, x_grid, ln_g, ln_b, w_qk, out_0, 
         project(1, 0)
         statistics(6)
         pass_through(0, 0)
-        store(0, 0, False)
-        pack(1)
+        store(0, 0)
+        pack(1, nc.vector.tensor_copy)
+        quantise_x(1)
         project(0, 1)
         prepare_w_piece(8, nc.scalar.copy)
-        rotate(1, 0, False)
+        rotate(1, 0)
         add_cross(1, 0)
         project(1, 1)
         prepare_w_piece(9, nc.scalar.copy)
@@ -418,69 +430,75 @@ def tile_transformerencoderlayer_pa_kernel(tc, x_grid, ln_g, ln_b, w_qk, out_0, 
         prepare_w_piece(11, nc.scalar.copy)
         normalise(2)
         pass_through(1, 0)
-        store(1, 0, False)
+        store(1, 0)
         statistics(7)
-        rotate(0, 1, False)
+        rotate(0, 1)
         add_cross(0, 1)
         flip(2)
         pass_through(0, 1)
-        store(0, 1, False)
-        rotate(1, 1, False)
+        store(0, 1)
+        rotate(1, 1)
         add_cross(1, 1)
         quantise_w(2)
         project(2, 0)
         pass_through(1, 1)
-        store(1, 1, False)
+        store(1, 1)
         prepare_w_piece(12, nc.scalar.copy)
         prepare_w_piece(13, nc.scalar.copy)
-        pack(2)
+        pack(2, nc.vector.tensor_copy)
+        quantise_x(2)
         project(2, 1)
-        rotate(2, 0, False)
+        rotate(2, 0)
         add_cross(2, 0)
         prepare_w_piece(14, nc.scalar.copy)
         prepare_w_piece(15, nc.scalar.copy)
         project(0, 2)
         normalise(3)
         pass_through(2, 0)
-        store(2, 0, False)
-        rotate(2, 1, False)
+        store(2, 0)
+        rotate(2, 1)
         add_cross(2, 1)
         flip(3)
         project(1, 2)
         pass_through(2, 1)
-        store(2, 1, False)
-        rotate(0, 2, False)
+        store(2, 1)
+        prepare_w_piece(16, nc.scalar.copy)
+        rotate(0, 2)
         add_cross(0, 2)
-        quantise_w(3)
+        pack(3, nc.scalar.copy)
         project(2, 2)
-        rotate(1, 2, False)
+        prepare_w_piece(17, nc.scalar.copy)
+        rotate(1, 2)
         add_cross(1, 2)
         pass_through(0, 2)
-        store(0, 2, False)
-        pass_through(1, 2)
-        store(1, 2, False)
-        prepare_w_piece(16, nc.scalar.copy)
-        pack(3)
+        store(0, 2)
+        quantise_w(3)
+        quantise_x(3)
+        prepare_w_piece(18, nc.scalar.copy)
         project(3, 0)
-        rotate(2, 2, False)
+        pass_through(1, 2)
+        store(1, 2)
+        rotate(2, 2)
         add_cross(2, 2)
         project(3, 1)
         pass_through(2, 2)
-        store(2, 2, False)
-        prepare_w_piece(17, nc.scalar.copy)
-        steps = [(3, 0), (3, 1), (3, 2), (0, 3), (1, 3), (2, 3), (3, 3)] + [(head, pair) for head in range(4, HEADS) for pair in range(PAIRS)]
-        piece = 4 * W_PIECES + 2
-        for step in range(0, len(steps)):
-            last = step == len(steps) - 1
-            if not last and step > 0:
+        store(2, 2)
+        steps = [(3, 0), (3, 1), (3, 2), (0, 3), (1, 3), (2, 3), (3, 3)]
+        steps += [(head, pair) for head in range(FIRST_LONG_HEAD, HEADS) for pair in range(PAIRS)]
+        piece = 4 * W_PIECES + 3
+        for step, (head, pair) in enumerate(steps):
+            if 0 < step < len(steps) - 1:
                 project(*steps[step + 1])
             if piece < HEADS * W_PIECES:
                 prepare_w_piece(piece, nc.scalar.copy)
-            rotate(*steps[step], last)
-            pass_through(*steps[step])
-            if not last:
-                add_cross(*steps[step])
-            store(*steps[step], last)
+            rotate(head, pair)
+            pass_through(head, pair)
+            run, part = place(head, pair)
+            if step == len(steps) - 1:
+                add_and_store_last(head, run)
+            elif (part + 1) * PAIR == run_tiles(head):
+                add_cross(head, run)
+                store(head, run)
             piece += 1
             if piece % W_PIECES == 0 and piece <= HEADS * W_PIECES:
                 quantise_w(piece // W_PIECES - 1)

@@ -42,10 +42,10 @@ W_PIECES = PASSES * HALVES
 
 ROUND_MAGIC = 12582912.0
 
-NORMALISED_ON_VECTOR = (0,)
+NORMALISED_ON_VECTOR = (0, 3)
 
 FIRST_LONG_HEAD = 4
-Y_BUFS = {2: 4, 4: 3}
+Y_BUFS = {2: 4, 4: 4}
 CROSS_BUFS = {2: 3, 4: 2}
 
 FLOPS = 2 * TOKENS * FEATURES * HEADS * CHANNELS

@@ -293,8 +293,8 @@ def tile_transformerencoderlayer_pa_kernel(tc, x_grid, ln_g, ln_b, w_qk, out_0, 
                     [P, PASSES, CHANNELS, PACK], BF16, align_bytes=64, name="w_grouped"
                 )
             copy(
-                out=w_grouped[head][:, g, cols, :].rearrange("p (c i) t -> p c t i", i=4),
-                in_=w_raw[head][:, g, :, cols].rearrange("p t (c i) -> p c t i", i=4),
+                out=w_grouped[head][:, g, cols, :].rearrange("p (c i) t -> p c t i", i=8),
+                in_=w_raw[head][:, g, :, cols].rearrange("p t (c i) -> p c t i", i=8),
             )
 
         def quantise_w(head):

@@ -102,22 +102,8 @@ def tile_transformerencoderlayer_pa_kernel(tc, x_grid, ln_g, ln_b, w_qk, out_0, 
         ratio = (MAX_FREQ / 2.0) ** (1.0 / (FREQS - 1))
         coarse = keep.tile([P, 16], F32)
         fine = keep.tile([P, 16], F32)
-        nc.gpsimd.memset(coarse[:, 0:1], 1.0)
+        nc.vector.memset(coarse[:, 0:1], 1.0)
         nc.vector.memset(fine[:, 0:1], 1.0)
-        for doubling in range(4):
-            filled = 2**doubling
-            nc.gpsimd.tensor_scalar(
-                out=coarse[:, filled : 2 * filled],
-                in0=coarse[:, 0:filled],
-                scalar1=ratio ** (10 * filled),
-                scalar2=0.0,
-                op0=ALU.mult,
-                op1=ALU.add,
-            )
-            nc.vector.tensor_scalar_mul(
-                out=fine[:, filled : 2 * filled], in0=fine[:, 0:filled], scalar1=ratio**filled
-            )
-        freq = keep.tile([P, FREQS], F32)
         minus_half = keep.tile([P, PAIR], F32)
         nc.gpsimd.memset(minus_half[:], -0.5)
         ident = keep.tile([P, P], F32)
@@ -125,16 +111,26 @@ def tile_transformerencoderlayer_pa_kernel(tc, x_grid, ln_g, ln_b, w_qk, out_0, 
         gain = keep.tile([P, CHUNKS], F32)
         bias = keep.tile([P, CHUNKS], F32)
 
+        def double(doubling):
+            filled = 2**doubling
+            for table, step in ((coarse, 10), (fine, 1)):
+                nc.vector.tensor_scalar_mul(
+                    out=table[:, filled : 2 * filled], in0=table[:, 0:filled], scalar1=ratio ** (step * filled)
+                )
+
         blocks = TILES + 1
         grid_index = keep.tile([P, blocks], I32)
+        coord = keep.tile([P, blocks], F32)
         nc.vector.tensor_single_scalar(
             out=grid_index[:, 0:1], in_=token[:, 0:1], scalar=5, op=ALU.arith_shift_right
         )
+        double(0)
         nc.vector.tensor_single_scalar(out=grid_index[:, 1:blocks], in_=token[:], scalar=GRID - 1, op=ALU.bitwise_and)
-        coord = keep.tile([P, blocks], F32)
+        double(1)
         nc.vector.tensor_scalar(
             out=coord[:, 0:1], in0=grid_index[:, 0:1], scalar1=-1.0 / (GRID - 1), scalar2=0.5, op0=ALU.mult, op1=ALU.add
         )
+        double(2)
         nc.vector.tensor_scalar(
             out=coord[:, 1:blocks],
             in0=grid_index[:, 1:blocks],
@@ -143,6 +139,8 @@ def tile_transformerencoderlayer_pa_kernel(tc, x_grid, ln_g, ln_b, w_qk, out_0, 
             op0=ALU.mult,
             op1=ALU.add,
         )
+        double(3)
+        freq = keep.tile([P, FREQS], F32)
         nc.vector.tensor_tensor(
             out=freq[:].rearrange("p (a b) -> p a b", b=10),
             in0=coarse[:, 0:10].unsqueeze(2).to_broadcast([P, 10, 10]),
@@ -193,16 +191,20 @@ def tile_transformerencoderlayer_pa_kernel(tc, x_grid, ln_g, ln_b, w_qk, out_0, 
         rstd = {}
         shift = {}
 
-        def statistics(i):
+        stats = {}
+
+        def gather(i, part):
+            if part == 0:
+                stats[i] = small.tile([P, FEATURES // BN_WIDTH, 6], F32, name="stats")
+            nc.vector.bn_stats(
+                out=stats[i][:, part, :], in_=x_sb[:, i, part * BN_WIDTH : (part + 1) * BN_WIDTH]
+            )
+
+        def merge(i):
             pair, a = divmod(i, PAIR)
             if a == 0:
                 mean_var[pair] = small.tile([P, PAIR, 2], F32, name="mean_var")
-            stats = small.tile([P, FEATURES // BN_WIDTH, 6], F32)
-            for part in range(FEATURES // BN_WIDTH):
-                nc.vector.bn_stats(
-                    out=stats[:, part, :], in_=x_sb[:, i, part * BN_WIDTH : (part + 1) * BN_WIDTH]
-                )
-            nc.vector.bn_aggr(out=mean_var[pair][:, a, :], in_=stats[:].rearrange("p a s -> p (a s)"))
+            nc.vector.bn_aggr(out=mean_var[pair][:, a, :], in_=stats[i][:].rearrange("p a s -> p (a s)"))
             if a == PAIR - 1:
                 scale_of(pair)
 
@@ -293,8 +295,8 @@ def tile_transformerencoderlayer_pa_kernel(tc, x_grid, ln_g, ln_b, w_qk, out_0, 
                     [P, PASSES, CHANNELS, PACK], BF16, align_bytes=64, name="w_grouped"
                 )
             copy(
-                out=w_grouped[head][:, g, cols, :].rearrange("p (c i) t -> p c t i", i=8),
-                in_=w_raw[head][:, g, :, cols].rearrange("p t (c i) -> p c t i", i=8),
+                out=w_grouped[head][:, g, cols, :].rearrange("p (c i) t -> p c t i", i=4),
+                in_=w_raw[head][:, g, :, cols].rearrange("p t (c i) -> p c t i", i=4),
             )
 
         def quantise_w(head):
@@ -388,19 +390,29 @@ def tile_transformerencoderlayer_pa_kernel(tc, x_grid, ln_g, ln_b, w_qk, out_0, 
 
         fold_angles(slice(0, blocks))
         make_tables(slice(0, blocks))
-        statistics(0)
-        statistics(1)
+        gather(0, 0)
+        gather(0, 1)
+        gather(1, 0)
+        gather(1, 1)
+        merge(0)
+        gather(2, 0)
+        merge(1)
         load_gain_and_bias()
         prepare_w_piece(0, nc.scalar.copy)
         prepare_w_piece(2, nc.scalar.copy)
-        statistics(2)
+        gather(2, 1)
+        gather(3, 0)
         normalise(0)
         flip(0)
-        statistics(3)
+        gather(3, 1)
+        merge(2)
         prepare_w_piece(1, nc.vector.tensor_copy)
         prepare_w_piece(3, nc.vector.tensor_copy)
+        merge(3)
         quantise_w(0)
+        gather(4, 0)
         pack(0, nc.vector.tensor_copy)
+        gather(4, 1)
         quantise_x(0)
         project(0, 0)
         prepare_w_piece(4, nc.scalar.copy)
@@ -408,17 +420,21 @@ def tile_transformerencoderlayer_pa_kernel(tc, x_grid, ln_g, ln_b, w_qk, out_0, 
         normalise(1)
         prepare_w_piece(6, nc.scalar.copy)
         prepare_w_piece(7, nc.scalar.copy)
-        statistics(4)
+        gather(5, 0)
+        merge(4)
+        gather(5, 1)
         rotate(0, 0)
         add_cross(0, 0)
         flip(1)
-        statistics(5)
+        gather(6, 0)
+        merge(5)
         quantise_w(1)
         project(1, 0)
-        statistics(6)
+        gather(6, 1)
         pass_through(0, 0)
         store(0, 0)
         pack(1, nc.vector.tensor_copy)
+        merge(6)
         quantise_x(1)
         project(0, 1)
         prepare_w_piece(8, nc.scalar.copy)
@@ -431,7 +447,8 @@ def tile_transformerencoderlayer_pa_kernel(tc, x_grid, ln_g, ln_b, w_qk, out_0, 
         normalise(2)
         pass_through(1, 0)
         store(1, 0)
-        statistics(7)
+        gather(7, 0)
+        gather(7, 1)
         rotate(0, 1)
         add_cross(0, 1)
         flip(2)
@@ -446,6 +463,7 @@ def tile_transformerencoderlayer_pa_kernel(tc, x_grid, ln_g, ln_b, w_qk, out_0, 
         prepare_w_piece(12, nc.scalar.copy)
         prepare_w_piece(13, nc.scalar.copy)
         pack(2, nc.vector.tensor_copy)
+        merge(7)
         quantise_x(2)
         project(2, 1)
         rotate(2, 0)

@@ -83,13 +83,14 @@ def tile_transformerencoderlayer_pa_kernel(tc, x_grid, ln_g, ln_b, w_qk, out_0, 
                 nc.sync.dma_start(out=raw[:, g], in_=w_view[:, g, :, head * CHANNELS : (head + 1) * CHANNELS])
             w_raw.append(raw)
 
-        load_x(0)
+        for i in range(PAIR):
+            nc.sync.dma_start(out=x_sb[:, i, :], in_=x_view[:, i, :])
+        load_x(1)
+        load_w(0)
         gain_raw = keep.tile([P, PASSES, PACK], BF16)
         bias_raw = keep.tile([P, PASSES, PACK], BF16)
         nc.sync.dma_start(out=gain_raw[:], in_=ln_g.rearrange("(g p t) -> p g t", p=P, t=PACK))
         nc.sync.dma_start(out=bias_raw[:], in_=ln_b.rearrange("(g p t) -> p g t", p=P, t=PACK))
-        load_x(1)
-        load_w(0)
         load_w(1)
         load_x(2)
         load_x(3)

@@ -449,7 +449,6 @@ def tile_transformerencoderlayer_pa_kernel(tc, x_grid, ln_g, ln_b, w_qk, out_0, 
         pass_through(1, 0)
         store(1, 0)
         gather(7, 0)
-        gather(7, 1)
         rotate(0, 1)
         add_cross(0, 1)
         flip(2)
@@ -459,6 +458,7 @@ def tile_transformerencoderlayer_pa_kernel(tc, x_grid, ln_g, ln_b, w_qk, out_0, 
         add_cross(1, 1)
         quantise_w(2)
         project(2, 0)
+        gather(7, 1)
         pass_through(1, 1)
         store(1, 1)
         prepare_w_piece(12, nc.scalar.copy)
@@ -477,11 +477,11 @@ def tile_transformerencoderlayer_pa_kernel(tc, x_grid, ln_g, ln_b, w_qk, out_0, 
         store(2, 0)
         rotate(2, 1)
         add_cross(2, 1)
+        prepare_w_piece(16, nc.scalar.copy)
         flip(3)
         project(1, 2)
         pass_through(2, 1)
         store(2, 1)
-        prepare_w_piece(16, nc.scalar.copy)
         rotate(0, 2)
         add_cross(0, 2)
         pack(3, nc.scalar.copy)

import math
from contextlib import ExitStack

import concourse.mybir as mybir
from concourse.masks import make_identity

F32 = mybir.dt.float32
BF16 = mybir.dt.bfloat16
I32 = mybir.dt.int32
U32 = mybir.dt.uint32
U8 = mybir.dt.uint8
FP8X4 = mybir.dt.float8_e4m3fn_x4
ALU = mybir.AluOpType
ACT = mybir.ActivationFunctionType

P = 128
GRID = 32
TOKENS = GRID * GRID
FEATURES = 1024
HEADS = 8
HEADS_PER_OUTPUT = 4
CHANNELS = 512
FREQS = 100
HALF = 2 * FREQS
ROTATED = 2 * HALF
MAX_FREQ = 10.0
EPS = 1e-5

PACK = 4
K_PASS = P * PACK
PASSES = FEATURES // K_PASS
CHUNKS = FEATURES // P
TILES = TOKENS // P
PAIR = 2
PAIRS = TILES // PAIR
PAIR_TOKENS = PAIR * P
BN_WIDTH = 512

HALVES = 2
PIECE_CHANNELS = CHANNELS // HALVES
W_PIECES = PASSES * HALVES

ROUND_MAGIC = 12582912.0

NORMALISED_ON_VECTOR = (0, 3)

FIRST_LONG_HEAD = 4
Y_BUFS = {2: 4, 4: 4}
CROSS_BUFS = {2: 3, 4: 2}

FLOPS = 2 * TOKENS * FEATURES * HEADS * CHANNELS


def tile_transformerencoderlayer_pa_kernel(tc, x_grid, ln_g, ln_b, w_qk, out_0, out_1):
    nc = tc.nc
    with ExitStack() as ctx:
        keep = ctx.enter_context(tc.tile_pool(name="keep", bufs=1))
        small = ctx.enter_context(tc.tile_pool(name="small", bufs=PAIRS))
        hat_pool = ctx.enter_context(tc.tile_pool(name="hat", bufs=2))
        stage = ctx.enter_context(tc.tile_pool(name="stage", bufs=2))
        raw_pool = ctx.enter_context(tc.tile_pool(name="raw", bufs=6))
        grouped_pool = ctx.enter_context(tc.tile_pool(name="grouped", bufs=2))
        w_pool = ctx.enter_context(tc.tile_pool(name="w", bufs=5))
        y_pool = ctx.enter_context(tc.tile_pool(name="y", bufs=6))
        cross_pool = ctx.enter_context(tc.tile_pool(name="cross", bufs=4))
        flip_psum = ctx.enter_context(tc.psum_pool(name="flip", bufs=2))
        acc_psum = ctx.enter_context(tc.psum_pool(name="acc", bufs=6))

        ctx.enter_context(tc.manual_schedule())

        x_sb = keep.tile([P, TILES, FEATURES], BF16)
        x_view = x_grid[0].rearrange("(p i) d -> p i d", i=TILES)
        w_view = w_qk.rearrange("(g p t) n -> p g t n", t=PACK, p=P)
        w_raw = []

        def load_x(pair):
            tiles = slice(pair * PAIR, (pair + 1) * PAIR)
            nc.sync.dma_start(out=x_sb[:, tiles, :], in_=x_view[:, tiles, :])

        def load_w(head):
            raw = raw_pool.tile([P, PASSES, PACK, CHANNELS], BF16, name="w_raw")
            for g in range(PASSES):
                nc.sync.dma_start(out=raw[:, g], in_=w_view[:, g, :, head * CHANNELS : (head + 1) * CHANNELS])
            w_raw.append(raw)

        for i in range(PAIR):
            nc.sync.dma_start(out=x_sb[:, i, :], in_=x_view[:, i, :])
        load_x(1)
        load_w(0)
        gain_raw = keep.tile([P, PASSES, PACK], BF16)
        bias_raw = keep.tile([P, PASSES, PACK], BF16)
        nc.sync.dma_start(out=gain_raw[:], in_=ln_g.rearrange("(g p t) -> p g t", p=P, t=PACK))
        nc.sync.dma_start(out=bias_raw[:], in_=ln_b.rearrange("(g p t) -> p g t", p=P, t=PACK))
        load_w(1)
        load_x(2)
        load_x(3)
        for head in range(2, HEADS):
            load_w(head)

        token = keep.tile([P, TILES], I32)
        nc.gpsimd.iota(token[:], pattern=[[1, TILES]], base=0, channel_multiplier=TILES)

        ratio = (MAX_FREQ / 2.0) ** (1.0 / (FREQS - 1))
        coarse = keep.tile([P, 16], F32)
        fine = keep.tile([P, 16], F32)
        nc.vector.memset(coarse[:, 0:1], 1.0)
        nc.vector.memset(fine[:, 0:1], 1.0)
        minus_half = keep.tile([P, PAIR], F32)
        nc.gpsimd.memset(minus_half[:], -0.5)
        ident = keep.tile([P, P], F32)
        make_identity(nc, ident[:])
        gain = keep.tile([P, CHUNKS], F32)
        bias = keep.tile([P, CHUNKS], F32)

        def double(doubling):
            filled = 2**doubling
            for table, step in ((coarse, 10), (fine, 1)):
                nc.vector.tensor_scalar_mul(
                    out=table[:, filled : 2 * filled], in0=table[:, 0:filled], scalar1=ratio ** (step * filled)
                )

        blocks = TILES + 1
        grid_index = keep.tile([P, blocks], I32)
        coord = keep.tile([P, blocks], F32)
        nc.vector.tensor_single_scalar(
            out=grid_index[:, 0:1], in_=token[:, 0:1], scalar=5, op=ALU.arith_shift_right
        )
        double(0)
        nc.vector.tensor_single_scalar(out=grid_index[:, 1:blocks], in_=token[:], scalar=GRID - 1, op=ALU.bitwise_and)
        double(1)
        nc.vector.tensor_scalar(
            out=coord[:, 0:1], in0=grid_index[:, 0:1], scalar1=-1.0 / (GRID - 1), scalar2=0.5, op0=ALU.mult, op1=ALU.add
        )
        double(2)
        nc.vector.tensor_scalar(
            out=coord[:, 1:blocks],
            in0=grid_index[:, 1:blocks],
            scalar1=1.0 / (GRID - 1),
            scalar2=-0.5,
            op0=ALU.mult,
            op1=ALU.add,
        )
        double(3)
        freq = keep.tile([P, FREQS], F32)
        nc.vector.tensor_tensor(
            out=freq[:].rearrange("p (a b) -> p a b", b=10),
            in0=coarse[:, 0:10].unsqueeze(2).to_broadcast([P, 10, 10]),
            in1=fine[:, 0:10].unsqueeze(1).to_broadcast([P, 10, 10]),
            op=ALU.mult,
        )
        turn = keep.tile([P, blocks, FREQS], F32)
        rounded = keep.tile([P, blocks, FREQS], F32)
        back = keep.tile([P, blocks, FREQS], F32)
        cos_tab = keep.tile([P, blocks, FREQS], F32)
        sin_tab = keep.tile([P, blocks, FREQS], F32)

        def fold_angles(part):
            count = part.stop - part.start
            nc.vector.tensor_tensor(
                out=turn[:, part],
                in0=freq[:].unsqueeze(1).to_broadcast([P, count, FREQS]),
                in1=coord[:, part].unsqueeze(2).to_broadcast([P, count, FREQS]),
                op=ALU.mult,
            )
            nc.vector.tensor_scalar_add(out=rounded[:, part], in0=turn[:, part], scalar1=ROUND_MAGIC)
            nc.vector.scalar_tensor_tensor(
                out=back[:, part].rearrange("p b j -> p (b j)"),
                in0=rounded[:, part].rearrange("p b j -> p (b j)"),
                scalar=ROUND_MAGIC,
                in1=turn[:, part].rearrange("p b j -> p (b j)"),
                op0=ALU.subtract,
                op1=ALU.subtract,
            )

        def make_tables(part):
            two_pi = 2.0 * math.pi
            nc.scalar.activation(out=sin_tab[:, part], in_=back[:, part], func=ACT.Sin, scale=-two_pi)
            nc.scalar.activation(out=rounded[:, part], in_=back[:, part], func=ACT.Abs)
            nc.scalar.activation(
                out=cos_tab[:, part], in_=rounded[:, part], func=ACT.Sin, scale=-two_pi, bias=math.pi / 2.0
            )

        x_codes = keep.tile([P, PAIRS, PASSES, PAIR_TOKENS], U32, align_bytes=64)
        x_scales = keep.tile([P, PAIRS, PASSES, PAIR_TOKENS], U8, align_bytes=64)
        x_hat = {}

        def load_gain_and_bias():
            nc.gpsimd.tensor_copy(out=gain[:], in_=gain_raw[:].rearrange("p g t -> p (g t)"))
            nc.gpsimd.tensor_copy(out=bias[:], in_=bias_raw[:].rearrange("p g t -> p (g t)"))

        mean_var = {}
        rstd = {}
        shift = {}

        stats = {}

        def gather(i, part):
            if part == 0:
                stats[i] = small.tile([P, FEATURES // BN_WIDTH, 6], F32, name="stats")
            nc.vector.bn_stats(
                out=stats[i][:, part, :], in_=x_sb[:, i, part * BN_WIDTH : (part + 1) * BN_WIDTH]
            )

        def merge(i):
            pair, a = divmod(i, PAIR)
            if a == 0:
                mean_var[pair] = small.tile([P, PAIR, 2], F32, name="mean_var")
            nc.vector.bn_aggr(out=mean_var[pair][:, a, :], in_=stats[i][:].rearrange("p a s -> p (a s)"))
            if a == PAIR - 1:
                scale_of(pair)

        def scale_of(pair):
            var_eps = small.tile([P, PAIR], F32)
            nc.gpsimd.tensor_scalar(
                out=var_eps[:], in0=mean_var[pair][:, :, 1], scalar1=1.0, scalar2=EPS, op0=ALU.mult, op1=ALU.add
            )
            rstd[pair] = small.tile([P, PAIR], F32, name="rstd")
            nc.gpsimd.tensor_tensor(out=rstd[pair][:], in0=var_eps[:], in1=minus_half[:], op=ALU.pow)
            if pair not in NORMALISED_ON_VECTOR:
                minus_mean = small.tile([P, PAIR], F32)
                nc.gpsimd.tensor_scalar(
                    out=minus_mean[:], in0=mean_var[pair][:, :, 0], scalar1=-1.0, scalar2=0.0, op0=ALU.mult, op1=ALU.add
                )
                shift[pair] = small.tile([P, PAIR], F32, name="shift")
                nc.gpsimd.tensor_tensor(out=shift[pair][:], in0=minus_mean[:], in1=rstd[pair][:], op=ALU.mult)

        def normalise(pair):
            x_hat[pair] = hat_pool.tile([P, PAIR, PASSES, PACK, P], F32, name="x_hat")
            for a in range(PAIR):
                features = x_sb[:, pair * PAIR + a, :].rearrange("m (g p t) -> m g t p", g=PASSES, t=PACK)
                if pair in NORMALISED_ON_VECTOR:
                    nc.vector.tensor_scalar(
                        out=x_hat[pair][:, a],
                        in0=features,
                        scalar1=mean_var[pair][:, a, 0:1],
                        scalar2=rstd[pair][:, a : a + 1],
                        op0=ALU.subtract,
                        op1=ALU.mult,
                    )
                else:
                    nc.scalar.activation(
                        out=x_hat[pair][:, a],
                        in_=features,
                        func=ACT.Identity,
                        scale=rstd[pair][:, a : a + 1],
                        bias=shift[pair][:, a : a + 1],
                    )

        xn_t = {}

        def flip(pair):
            xn_t[pair] = stage.tile([P, CHUNKS, PAIR_TOKENS], BF16, name="xn_t")
            for c in range(0, CHUNKS, 2):
                flipped = flip_psum.tile([P, 2, PAIR, P], F32, tag="flipped")
                for b in range(2):
                    for a in range(PAIR):
                        nc.tensor.transpose(
                            flipped[:, b, a, :], x_hat[pair][:, a, (c + b) // PACK, (c + b) % PACK, :], ident[:]
                        )
                for b in range(2):
                    nc.scalar.activation(
                        out=xn_t[pair][:, c + b, :],
                        in_=flipped[:, b].rearrange("p a m -> p (a m)"),
                        func=ACT.Identity,
                        scale=gain[:, c + b : c + b + 1],
                        bias=bias[:, c + b : c + b + 1],
                    )

        def pack(pair, copy):
            xn_grouped = stage.tile([P, PASSES, PAIR_TOKENS, PACK], BF16, align_bytes=64, name="xn_grouped")
            copy(
                out=xn_grouped[:].rearrange("p g (c i) t -> p g c t i", i=4),
                in_=xn_t[pair][:].rearrange("p (g t) (c i) -> p g c t i", t=PACK, i=4),
            )
            grouped_x[pair] = xn_grouped

        grouped_x = {}

        def quantise_x(pair):
            nc.vector.quantize_mx(
                out=x_codes[:, pair].rearrange("p g m -> p (g m)").bitcast(FP8X4),
                scales=x_scales[:, pair].rearrange("p g m -> p (g m)"),
                in_=grouped_x[pair][:].rearrange("p g m t -> p (g m t)"),
            )

        w_grouped = {}
        w_codes = {}
        w_scales = {}

        def prepare_w_piece(number, copy):
            head, piece = divmod(number, W_PIECES)
            g, half = divmod(piece, HALVES)
            cols = slice(half * PIECE_CHANNELS, (half + 1) * PIECE_CHANNELS)
            if piece == 0:
                w_grouped[head] = grouped_pool.tile(
                    [P, PASSES, CHANNELS, PACK], BF16, align_bytes=64, name="w_grouped"
                )
            copy(
                out=w_grouped[head][:, g, cols, :].rearrange("p (c i) t -> p c t i", i=4),
                in_=w_raw[head][:, g, :, cols].rearrange("p t (c i) -> p c t i", i=4),
            )

        def quantise_w(head):
            w_codes[head] = w_pool.tile([P, PASSES, CHANNELS], U32, align_bytes=64, name="w_codes")
            w_scales[head] = w_pool.tile([P, PASSES, CHANNELS], U8, align_bytes=64, name="w_scales")
            nc.vector.quantize_mx(
                out=w_codes[head][:].rearrange("p g c -> p (g c)").bitcast(FP8X4),
                scales=w_scales[head][:].rearrange("p g c -> p (g c)"),
                in_=w_grouped[head][:].rearrange("p g c t -> p (g c t)"),
            )

        u = {}

        def run_tiles(head):
            return 2 * PAIR if head >= FIRST_LONG_HEAD else PAIR

        def place(head, pair):
            return divmod(pair, run_tiles(head) // PAIR)

        def project(head, pair):
            for a in range(PAIR):
                tile_cols = slice(a * P, (a + 1) * P)
                acc = acc_psum.tile([P, CHANNELS], F32)
                for g in range(PASSES):
                    nc.tensor.matmul_mx(
                        out=acc[:],
                        lhsT=x_codes[:, pair, g, tile_cols].bitcast(FP8X4),
                        lhsT_scale=x_scales[:, pair, g, tile_cols],
                        rhs=w_codes[head][:, g, :].bitcast(FP8X4),
                        rhs_scale=w_scales[head][:, g, :],
                        start=(g == 0),
                        stop=(g == PASSES - 1),
                    )
                u[head, pair * PAIR + a] = acc

        y = {}
        crosses = {}

        def pass_through(head, pair):
            run, part = place(head, pair)
            for a in range(PAIR):
                nc.scalar.copy(
                    out=y[head, run][:, part * PAIR + a, ROTATED:CHANNELS], in_=u[head, pair * PAIR + a][:, ROTATED:CHANNELS]
                )

        def rotate(head, pair):
            run, part = place(head, pair)
            if part == 0:
                tiles = run_tiles(head)
                y[head, run] = y_pool.tile([P, tiles, CHANNELS], F32, name="y%d" % tiles, bufs=Y_BUFS[tiles])
                crosses[head, run] = cross_pool.tile([P, tiles, ROTATED], F32, name="cross%d" % tiles, bufs=CROSS_BUFS[tiles])
            y_pair = y[head, run][:, part * PAIR : (part + 1) * PAIR]
            cross = crosses[head, run][:, part * PAIR : (part + 1) * PAIR]
            for a in range(PAIR):
                i = pair * PAIR + a
                cos_in = cos_tab[:, 0 : i + 2 : i + 1, :].unsqueeze(3).to_broadcast([P, 2, FREQS, 2])
                sin_in = sin_tab[:, 0 : i + 2 : i + 1, :].unsqueeze(3).to_broadcast([P, 2, FREQS, 2])
                nc.vector.tensor_tensor(
                    out=y_pair[:, a, 0:ROTATED].rearrange("p (b j d) -> p b j d", b=2, d=2),
                    in0=u[head, i][:, 0:ROTATED].rearrange("p (b j d) -> p b j d", b=2, d=2),
                    in1=cos_in,
                    op=ALU.mult,
                )
                nc.vector.tensor_tensor(
                    out=cross[:, a, :].rearrange("p (b j d) -> p b j d", b=2, d=2),
                    in0=u[head, i][:, 0:ROTATED].rearrange("p (j d e) -> p e j d", d=2, e=2)[:, ::-1],
                    in1=sin_in,
                    op=ALU.mult,
                )

        def add_cross(head, run):
            y_run = y[head, run][:, :, 0:ROTATED]
            nc.gpsimd.tensor_tensor(out=y_run, in0=y_run, in1=crosses[head, run][:], op=ALU.add)

        def run_slice(head, run):
            out_tensor = out_0 if head < HEADS_PER_OUTPUT else out_1
            tiles = run_tiles(head)
            out_head = out_tensor[0, head % HEADS_PER_OUTPUT].rearrange("(p i) c -> p i c", i=TILES)
            return out_head[:, run * tiles : (run + 1) * tiles, :]

        def store(head, run):
            nc.sync.dma_start(out=run_slice(head, run), in_=y[head, run][:])

        def add_and_store_last(head, run):
            for a in range(run_tiles(head)):
                y_tile = y[head, run][:, a, :]
                nc.vector.tensor_tensor(
                    out=y_tile[:, 0:ROTATED], in0=y_tile[:, 0:ROTATED], in1=crosses[head, run][:, a, :], op=ALU.add
                )
                nc.sync.dma_start(out=run_slice(head, run)[:, a, :], in_=y_tile)

        fold_angles(slice(0, blocks))
        make_tables(slice(0, blocks))
        gather(0, 0)
        gather(0, 1)
        gather(1, 0)
        gather(1, 1)
        merge(0)
        gather(2, 0)
        merge(1)
        load_gain_and_bias()
        prepare_w_piece(0, nc.scalar.copy)
        prepare_w_piece(2, nc.scalar.copy)
        gather(2, 1)
        gather(3, 0)
        normalise(0)
        flip(0)
        gather(3, 1)
        merge(2)
        prepare_w_piece(1, nc.vector.tensor_copy)
        prepare_w_piece(3, nc.vector.tensor_copy)
        merge(3)
        quantise_w(0)
        gather(4, 0)
        pack(0, nc.vector.tensor_copy)
        gather(4, 1)
        quantise_x(0)
        project(0, 0)
        prepare_w_piece(4, nc.scalar.copy)
        prepare_w_piece(5, nc.scalar.copy)
        normalise(1)
        prepare_w_piece(6, nc.scalar.copy)
        prepare_w_piece(7, nc.scalar.copy)
        gather(5, 0)
        merge(4)
        gather(5, 1)
        rotate(0, 0)
        add_cross(0, 0)
        flip(1)
        gather(6, 0)
        merge(5)
        quantise_w(1)
        project(1, 0)
        gather(6, 1)
        pass_through(0, 0)
        store(0, 0)
        pack(1, nc.vector.tensor_copy)
        merge(6)
        quantise_x(1)
        project(0, 1)
        prepare_w_piece(8, nc.scalar.copy)
        rotate(1, 0)
        add_cross(1, 0)
        project(1, 1)
        prepare_w_piece(9, nc.scalar.copy)
        prepare_w_piece(10, nc.scalar.copy)
        prepare_w_piece(11, nc.scalar.copy)
        normalise(2)
        pass_through(1, 0)
        store(1, 0)
        gather(7, 0)
        rotate(0, 1)
        add_cross(0, 1)
        flip(2)
        pass_through(0, 1)
        store(0, 1)
        rotate(1, 1)
        add_cross(1, 1)
        quantise_w(2)
        project(2, 0)
        gather(7, 1)
        pass_through(1, 1)
        store(1, 1)
        prepare_w_piece(12, nc.scalar.copy)
        prepare_w_piece(13, nc.scalar.copy)
        pack(2, nc.vector.tensor_copy)
        merge(7)
        quantise_x(2)
        project(2, 1)
        rotate(2, 0)
        add_cross(2, 0)
        prepare_w_piece(14, nc.scalar.copy)
        prepare_w_piece(15, nc.scalar.copy)
        project(0, 2)
        normalise(3)
        pass_through(2, 0)
        store(2, 0)
        rotate(2, 1)
        add_cross(2, 1)
        prepare_w_piece(16, nc.scalar.copy)
        flip(3)
        project(1, 2)
        pass_through(2, 1)
        store(2, 1)
        rotate(0, 2)
        add_cross(0, 2)
        pack(3, nc.scalar.copy)
        project(2, 2)
        prepare_w_piece(17, nc.scalar.copy)
        rotate(1, 2)
        add_cross(1, 2)
        pass_through(0, 2)
        store(0, 2)
        quantise_w(3)
        quantise_x(3)
        prepare_w_piece(18, nc.scalar.copy)
        project(3, 0)
        pass_through(1, 2)
        store(1, 2)
        rotate(2, 2)
        add_cross(2, 2)
        project(3, 1)
        pass_through(2, 2)
        store(2, 2)
        steps = [(3, 0), (3, 1), (3, 2), (0, 3), (1, 3), (2, 3), (3, 3)]
        steps += [(head, pair) for head in range(FIRST_LONG_HEAD, HEADS) for pair in range(PAIRS)]
        piece = 4 * W_PIECES + 3
        for step, (head, pair) in enumerate(steps):
            if 0 < step < len(steps) - 1:
                project(*steps[step + 1])
            if piece < HEADS * W_PIECES:
                prepare_w_piece(piece, nc.scalar.copy)
            rotate(head, pair)
            pass_through(head, pair)
            run, part = place(head, pair)
            if step == len(steps) - 1:
                add_and_store_last(head, run)
            elif (part + 1) * PAIR == run_tiles(head):
                add_cross(head, run)
                store(head, run)
            piece += 1
            if piece % W_PIECES == 0 and piece <= HEADS * W_PIECES:
                quantise_w(piece // W_PIECES - 1)
